import numpy as np
import ml_dtypes

BF16 = ml_dtypes.bfloat16


def bf(x):
    return np.asarray(x, np.float32).astype(BF16)


def f32(x):
    return np.asarray(x, np.float32)


def f64(x):
    return np.asarray(x).astype(np.float64)


def striped(idx):
    return np.tile(idx.reshape(-1, 16).T, (8, 1))


R, T, D, B, H, S, N = 3, 128, 512, 8, 256, 4096, 2048
QK, VS, BI, BS = 1.2, 2.0, 0.3, 0.5


def setup_inputs():
    return {
        "x": bf(np.random.standard_normal((R, T, N))),
        "w_u": bf(np.random.standard_normal((T, D)) / np.sqrt(T)),
        "b_u": f32(BI * np.random.standard_normal((D, 1))),
        "wq": bf(QK * np.random.standard_normal((D, D)) / np.sqrt(D)),
        "bq": f32(BI * np.random.standard_normal((D, 1))),
        "wk": bf(QK * np.random.standard_normal((D, D)) / np.sqrt(D)),
        "wv": bf(VS * np.random.standard_normal((D, D)) / np.sqrt(D)),
        "bv": f32(BI * np.random.standard_normal((D, 1))),
        "base": f32(BS * np.random.standard_normal((D, S))),
        "offs": striped(np.random.permutation(S)[:N]),
    }


def reference(x, w_u, b_u, wq, bq, wk, wv, bv, base, offs):
    idx = offs[:16].T.reshape(-1)
    h = [f64(w_u).T @ f64(x)[i] + f64(b_u) for i in range(R)]
    q = f64(wq).T @ h[0] + f64(bq)
    k = f64(wk).T @ h[1]
    v = f64(wv).T @ h[2] + f64(bv)
    q3 = q.reshape(D, B, H).transpose(1, 2, 0)
    k3 = k.reshape(D, B, H).transpose(1, 0, 2)
    v3 = v.reshape(D, B, H).transpose(1, 2, 0)
    p = np.exp((q3 @ k3) / np.sqrt(D))
    den = p.sum(axis=-1)
    num = p @ v3
    att = num * (1.0 / den)[:, :, None]
    res = f64(base).copy()
    res[:, idx] = att.reshape(N, D).T
    return res

@@ -1,0 +1,198 @@
+import math
+
+import concourse.mybir as mybir
+from concourse.masks import make_identity
+
+BF16, F32, U16 = mybir.dt.bfloat16, mybir.dt.float32, mybir.dt.uint16
+ACT = mybir.ActivationFunctionType
+ALU = mybir.AluOpType
+AXIS = mybir.AxisListType
+
+P = 128
+STREAMS = 3
+TOKENS = 2048
+D = 512
+DB = D // P
+SLOTS = 4096
+USER = 256
+CHUNK = 512
+HALF = 1024
+SCALE = 1.0 / math.sqrt(D)
+
+FLOPS = 2 * (STREAMS * P * D * TOKENS + STREAMS * D * D * TOKENS + 2 * TOKENS * USER * D)
+
+
+def tile_nrmsmodel_b_kernel(tc, x, w_u, b_u, wq, bq, wk, wv, bv, base, offs, out):
+    nc = tc.nc
+    with (
+        tc.tile_pool(name="held", bufs=1) as held,
+        tc.tile_pool(name="hidden", bufs=8) as hidden,
+        tc.tile_pool(name="work", bufs=3) as work,
+        tc.psum_pool(name="psum", bufs=2) as psum,
+    ):
+        offsets = held.tile([P, TOKENS // 16], U16, name="offsets")
+        nc.sync.dma_start(offsets[:], offs)
+
+        w_u_sb = held.tile([P, D], BF16, name="w_u_sb")
+        nc.sync.dma_start(w_u_sb[:], w_u)
+        x_sb = [held.tile([P, TOKENS], BF16, name=f"x_sb{i}") for i in range(STREAMS)]
+
+        def load_x(i, half):
+            cols = slice(half * HALF, (half + 1) * HALF)
+            nc.sync.dma_start(x_sb[i][:, cols], x[i, :, cols])
+
+        def load_bias(bias, name):
+            tile = held.tile([P, DB], F32, name=name)
+            nc.sync.dma_start(tile[:], bias.rearrange("(p b) one -> p (b one)", b=DB))
+            return tile
+
+        def load_weight(w, name):
+            tile = held.tile([P, DB, D], BF16, name=name)
+            nc.sync.dma_start(tile[:], w.rearrange("(p kb) d -> p kb d", kb=DB))
+            return tile
+
+        load_x(0, 0)
+        load_x(1, 0)
+        b_u_sb = load_bias(b_u, "b_u_sb")
+        wq_sb = load_weight(wq, "wq_sb")
+        bq_sb = load_bias(bq, "bq_sb")
+        wk_sb = load_weight(wk, "wk_sb")
+        load_x(2, 0)
+        wv_sb = load_weight(wv, "wv_sb")
+        bv_sb = held.tile([P, D], F32, name="bv_sb")
+        nc.sync.dma_start(bv_sb[:], bv.rearrange("c one -> (c one)").partition_broadcast(P))
+        for i in range(STREAMS):
+            load_x(i, 1)
+        window = [held.tile([P, SLOTS], F32, name=f"window{c}") for c in range(DB)]
+        for c in range(DB):
+            nc.sync.dma_start(window[c][:], base[c * P : (c + 1) * P, :])
+
+        ident_bf = held.tile([P, P], BF16, name="ident_bf")
+        make_identity(nc, ident_bf[:])
+        ident_f = held.tile([P, P], F32, name="ident_f")
+        make_identity(nc, ident_f[:])
+
+        w_u_blocks = w_u_sb[:].rearrange("f (p b) -> f b p", b=DB)
+        wq_blocks = wq_sb[:].rearrange("a kb (p b) -> a kb b p", b=DB)
+        wk_blocks = wk_sb[:].rearrange("a kb (p b) -> a kb b p", b=DB)
+
+        q_sb = held.tile([P, DB, TOKENS], BF16, name="q_sb")
+        k_sb = held.tile([P, DB, TOKENS], BF16, name="k_sb")
+        vT_sb = held.tile([P, TOKENS // P, D], BF16, name="vT_sb")
+        pT_sb = held.tile([P, TOKENS // USER, 2, USER], BF16, name="pT_sb")
+        rden_sb = held.tile([P, TOKENS], F32, name="rden_sb")
+
+        def project_h(i, t):
+            h = hidden.tile([P, DB, CHUNK], BF16, name="h")
+            for b in range(DB):
+                acc = psum.tile([P, CHUNK], F32, name="acc")
+                nc.tensor.matmul(acc[:], w_u_blocks[:, b, :], x_sb[i][:, t * CHUNK : (t + 1) * CHUNK])
+                nc.scalar.activation(h[:, b, :], acc[:], ACT.Identity, bias=b_u_sb[:, b : b + 1])
+            return h
+
+        def project_q(h, t):
+            for b in range(DB):
+                acc = psum.tile([P, CHUNK], F32, name="acc")
+                for kb in range(DB):
+                    nc.tensor.matmul(acc[:], wq_blocks[:, kb, b, :], h[:, kb, :], start=kb == 0, stop=kb == DB - 1)
+                nc.scalar.activation(
+                    q_sb[:, b, t * CHUNK : (t + 1) * CHUNK], acc[:], ACT.Identity, bias=bq_sb[:, b : b + 1]
+                )
+
+        def project_k(h, t, half):
+            for b in range(DB):
+                acc = psum.tile([P, CHUNK], F32, name="acc")
+                for kb in range(DB):
+                    nc.tensor.matmul(acc[:], wk_blocks[:, kb, b, :], h[:, kb, :], start=kb == 0, stop=kb == DB - 1)
+                if half == 0:
+                    nc.vector.tensor_copy(k_sb[:, b, t * CHUNK : (t + 1) * CHUNK], acc[:])
+                else:
+                    nc.scalar.copy(k_sb[:, b, t * CHUNK : (t + 1) * CHUNK], acc[:])
+
+        def project_v(h, t):
+            for s in range(CHUNK // P):
+                acc = psum.tile([P, D], F32, name="acc")
+                for kb in range(DB):
+                    nc.tensor.matmul(acc[:], h[:, kb, s * P : (s + 1) * P], wv_sb[:, kb, :], start=kb == 0, stop=kb == DB - 1)
+                nc.vector.tensor_tensor(vT_sb[:, t * (CHUNK // P) + s, :], acc[:], bv_sb[:], ALU.add)
+
+        def softmax(u):
+            tok = u * USER
+            scores = psum.tile([P, 2, USER], F32, name="scores")
+            for jb in range(2):
+                for b in range(DB):
+                    nc.tensor.matmul(
+                        scores[:, jb, :],
+                        q_sb[:, b, tok + jb * P : tok + (jb + 1) * P],
+                        k_sb[:, b, tok : tok + USER],
+                        start=b == 0,
+                        stop=b == DB - 1,
+                    )
+            top = work.tile([P, 2], F32, name="top")
+            nc.vector.reduce_max(top[:], scores[:], axis=AXIS.X)
+            shift = work.tile([P, 2], F32, name="shift")
+            nc.vector.tensor_scalar_mul(shift[:], top[:], -SCALE)
+            p_sb = work.tile([P, 2, USER], BF16, name="p_sb")
+            den = work.tile([P, 2], F32, name="den")
+            for jb in range(2):
+                nc.scalar.activation(
+                    p_sb[:, jb, :],
+                    scores[:, jb, :],
+                    ACT.Exp,
+                    bias=shift[:, jb : jb + 1],
+                    scale=SCALE,
+                    accum_out=den[:, jb : jb + 1],
+                )
+            pT_ps = psum.tile([P, 2, USER], BF16, name="pT_ps", tag="flipped")
+            for nb in range(2):
+                for jb in range(2):
+                    nc.tensor.transpose(
+                        pT_ps[:, nb, jb * P : (jb + 1) * P], p_sb[:, jb, nb * P : (nb + 1) * P], ident_bf[:]
+                    )
+            nc.vector.tensor_copy(pT_sb[:, u, :, :], pT_ps[:])
+            rcol = work.tile([P, 2], F32, name="rcol")
+            nc.vector.reciprocal(rcol[:], den[:])
+            spread = work.tile([P, 2, P], F32, name="spread")
+            nc.gpsimd.tensor_copy(spread[:], rcol[:].unsqueeze(2).to_broadcast([P, 2, P]))
+            r_ps = psum.tile([P, USER], F32, name="r_ps", tag="flipped")
+            for jb in range(2):
+                nc.tensor.transpose(r_ps[:, jb * P : (jb + 1) * P], spread[:, jb, :], ident_f[:])
+            nc.scalar.copy(rden_sb[:, tok : tok + USER], r_ps[:])
+
+        def attend_and_place(c, half):
+            num_sb = held.tile([P, HALF], F32, name=f"num_sb{c}_{half}")
+            for pair in range(HALF // CHUNK):
+                num_ps = psum.tile([P, CHUNK], F32, name="num_ps")
+                for s in range(CHUNK // USER):
+                    u = (half * HALF + pair * CHUNK) // USER + s
+                    for nb in range(2):
+                        nc.tensor.matmul(
+                            num_ps[:, s * USER : (s + 1) * USER],
+                            vT_sb[:, 2 * u + nb, c * P : (c + 1) * P],
+                            pT_sb[:, u, nb, :],
+                            start=nb == 0,
+                            stop=nb == 1,
+                        )
+                nc.scalar.copy(num_sb[:, pair * CHUNK : (pair + 1) * CHUNK], num_ps[:])
+            nc.vector.tensor_tensor(
+                window[c][:].indirect(offsets[:, half * (HALF // 16) : (half + 1) * (HALF // 16)]),
+                num_sb[:],
+                rden_sb[:, half * HALF : (half + 1) * HALF],
+                ALU.mult,
+            )
+
+        for half in range(TOKENS // HALF):
+            chunks = [half * (HALF // CHUNK) + s for s in range(HALF // CHUNK)]
+            for t in chunks:
+                h_q = project_h(0, t)
+                h_k = project_h(1, t)
+                project_q(h_q, t)
+                project_k(h_k, t, half)
+            for t in chunks:
+                project_v(project_h(2, t), t)
+            for u in range(half * (HALF // USER), (half + 1) * (HALF // USER)):
+                softmax(u)
+            for c in range(DB):
+                attend_and_place(c, half)
+                if half == TOKENS // HALF - 1:
+                    nc.sync.dma_start(out[c * P : (c + 1) * P, :], window[c][:])

@@ -22,11 +22,18 @@ SCALE = 1.0 / math.sqrt(D)
 FLOPS = 2 * (STREAMS * P * D * TOKENS + STREAMS * D * D * TOKENS + 2 * TOKENS * USER * D)
 
 
+def in_turn(*queues):
+    for i in range(max(len(queue) for queue in queues)):
+        for queue in queues:
+            if i < len(queue) and queue[i] is not None:
+                queue[i][0](*queue[i][1:])
+
+
 def tile_nrmsmodel_b_kernel(tc, x, w_u, b_u, wq, bq, wk, wv, bv, base, offs, out):
     nc = tc.nc
     with (
         tc.tile_pool(name="held", bufs=1) as held,
-        tc.tile_pool(name="hidden", bufs=8) as hidden,
+        tc.tile_pool(name="hidden", bufs=6) as hidden,
         tc.tile_pool(name="work", bufs=3) as work,
         tc.psum_pool(name="psum", bufs=2) as psum,
     ):
@@ -67,6 +74,10 @@ def tile_nrmsmodel_b_kernel(tc, x, w_u, b_u, wq, bq, wk, wv, bv, base, offs, out
         for c in range(DB):
             nc.sync.dma_start(window[c][:], base[c * P : (c + 1) * P, :])
 
+        warm = held.tile([P, 1], F32, name="warm")
+        nc.vector.memset(warm[:], 0.0)
+        nc.scalar.activation(warm[:], warm[:], ACT.Exp)
+
         ident_bf = held.tile([P, P], BF16, name="ident_bf")
         make_identity(nc, ident_bf[:])
         ident_f = held.tile([P, P], F32, name="ident_f")
@@ -81,118 +92,163 @@ def tile_nrmsmodel_b_kernel(tc, x, w_u, b_u, wq, bq, wk, wv, bv, base, offs, out
         vT_sb = held.tile([P, TOKENS // P, D], BF16, name="vT_sb")
         pT_sb = held.tile([P, TOKENS // USER, 2, USER], BF16, name="pT_sb")
         rden_sb = held.tile([P, TOKENS], F32, name="rden_sb")
+        num_sb = [
+            [held.tile([P, HALF], F32, name=f"num_sb{c}_{half}") for half in range(TOKENS // HALF)] for c in range(DB)
+        ]
 
-        def project_h(i, t):
-            h = hidden.tile([P, DB, CHUNK], BF16, name="h")
-            for b in range(DB):
-                acc = psum.tile([P, CHUNK], F32, name="acc")
-                nc.tensor.matmul(acc[:], w_u_blocks[:, b, :], x_sb[i][:, t * CHUNK : (t + 1) * CHUNK])
-                nc.scalar.activation(h[:, b, :], acc[:], ACT.Identity, bias=b_u_sb[:, b : b + 1])
-            return h
+        def copy_out(dst, src, t):
+            if t * CHUNK < HALF:
+                nc.vector.tensor_copy(dst, src)
+            else:
+                nc.scalar.copy(dst, src)
 
-        def project_q(h, t):
-            for b in range(DB):
-                acc = psum.tile([P, CHUNK], F32, name="acc")
-                for kb in range(DB):
-                    nc.tensor.matmul(acc[:], wq_blocks[:, kb, b, :], h[:, kb, :], start=kb == 0, stop=kb == DB - 1)
-                nc.scalar.activation(
-                    q_sb[:, b, t * CHUNK : (t + 1) * CHUNK], acc[:], ACT.Identity, bias=bq_sb[:, b : b + 1]
-                )
+        h_of = {}
 
-        def project_k(h, t, half):
-            for b in range(DB):
-                acc = psum.tile([P, CHUNK], F32, name="acc")
-                for kb in range(DB):
-                    nc.tensor.matmul(acc[:], wk_blocks[:, kb, b, :], h[:, kb, :], start=kb == 0, stop=kb == DB - 1)
-                if half == 0:
-                    nc.vector.tensor_copy(k_sb[:, b, t * CHUNK : (t + 1) * CHUNK], acc[:])
-                else:
-                    nc.scalar.copy(k_sb[:, b, t * CHUNK : (t + 1) * CHUNK], acc[:])
+        def hidden_block(i, t, b):
+            acc = psum.tile([P, CHUNK], F32, name="acc", bufs=3)
+            nc.tensor.matmul(acc[:], w_u_blocks[:, b, :], x_sb[i][:, t * CHUNK : (t + 1) * CHUNK])
+            if t * CHUNK < HALF and b % 2 == 1:
+                nc.vector.tensor_scalar_add(h_of[i, t][:, b, :], acc[:], b_u_sb[:, b : b + 1])
+            else:
+                nc.scalar.activation(h_of[i, t][:, b, :], acc[:], ACT.Identity, bias=b_u_sb[:, b : b + 1])
 
-        def project_v(h, t):
-            for s in range(CHUNK // P):
-                acc = psum.tile([P, D], F32, name="acc")
-                for kb in range(DB):
-                    nc.tensor.matmul(acc[:], h[:, kb, s * P : (s + 1) * P], wv_sb[:, kb, :], start=kb == 0, stop=kb == DB - 1)
-                nc.vector.tensor_tensor(vT_sb[:, t * (CHUNK // P) + s, :], acc[:], bv_sb[:], ALU.add)
+        def hidden_layer(i, t):
+            if t * CHUNK >= TOKENS:
+                return []
+            h_of[i, t] = hidden.tile([P, DB, CHUNK], BF16, name="h")
+            return [(hidden_block, i, t, b) for b in range(DB)]
 
-        def softmax(u):
+        def q_block(t, b):
+            acc = psum.tile([P, CHUNK], F32, name="acc", bufs=3)
+            for kb in range(DB):
+                nc.tensor.matmul(acc[:], wq_blocks[:, kb, b, :], h_of[0, t][:, kb, :], start=kb == 0, stop=kb == DB - 1)
+            nc.scalar.activation(q_sb[:, b, t * CHUNK : (t + 1) * CHUNK], acc[:], ACT.Identity, bias=bq_sb[:, b : b + 1])
+
+        def k_block(t, b):
+            acc = psum.tile([P, CHUNK], F32, name="acc", bufs=3)
+            for kb in range(DB):
+                nc.tensor.matmul(acc[:], wk_blocks[:, kb, b, :], h_of[1, t][:, kb, :], start=kb == 0, stop=kb == DB - 1)
+            copy_out(k_sb[:, b, t * CHUNK : (t + 1) * CHUNK], acc[:], t)
+
+        def v_block(t, s):
+            acc = psum.tile([P, D], F32, name="acc", bufs=3)
+            for kb in range(DB):
+                nc.tensor.matmul(acc[:], h_of[2, t][:, kb, s * P : (s + 1) * P], wv_sb[:, kb, :], start=kb == 0, stop=kb == DB - 1)
+            nc.vector.tensor_tensor(vT_sb[:, t * (CHUNK // P) + s, :], acc[:], bv_sb[:], ALU.add)
+
+        def project(block, t):
+            return [(block, t, b) for b in range(DB)]
+
+        scores_of, shift_of, p_of, spread_of = {}, {}, {}, {}
+
+        def scores(u):
             tok = u * USER
-            scores = psum.tile([P, 2, USER], F32, name="scores")
+            scores_of[u] = psum.tile([P, 2, USER], F32, name="scores")
             for jb in range(2):
                 for b in range(DB):
                     nc.tensor.matmul(
-                        scores[:, jb, :],
+                        scores_of[u][:, jb, :],
                         q_sb[:, b, tok + jb * P : tok + (jb + 1) * P],
                         k_sb[:, b, tok : tok + USER],
                         start=b == 0,
                         stop=b == DB - 1,
                     )
             top = work.tile([P, 2], F32, name="top")
-            nc.vector.reduce_max(top[:], scores[:], axis=AXIS.X)
-            shift = work.tile([P, 2], F32, name="shift")
-            nc.vector.tensor_scalar_mul(shift[:], top[:], -SCALE)
-            p_sb = work.tile([P, 2, USER], BF16, name="p_sb")
+            nc.vector.reduce_max(top[:], scores_of[u][:], axis=AXIS.X)
+            shift_of[u] = work.tile([P, 2], F32, name="shift")
+            nc.vector.tensor_scalar_mul(shift_of[u][:], top[:], -SCALE)
+
+        def weights(u):
+            p_of[u] = work.tile([P, 2, USER], BF16, name="p_sb")
             den = work.tile([P, 2], F32, name="den")
             for jb in range(2):
                 nc.scalar.activation(
-                    p_sb[:, jb, :],
-                    scores[:, jb, :],
+                    p_of[u][:, jb, :],
+                    scores_of[u][:, jb, :],
                     ACT.Exp,
-                    bias=shift[:, jb : jb + 1],
+                    bias=shift_of[u][:, jb : jb + 1],
                     scale=SCALE,
                     accum_out=den[:, jb : jb + 1],
                 )
-            pT_ps = psum.tile([P, 2, USER], BF16, name="pT_ps", tag="flipped")
+            rcol = work.tile([P, 2], F32, name="rcol")
+            nc.vector.reciprocal(rcol[:], den[:])
+            spread_of[u] = work.tile([P, 2, P], F32, name="spread")
+            nc.gpsimd.tensor_copy(spread_of[u][:], rcol[:].unsqueeze(2).to_broadcast([P, 2, P]))
+
+        def flip_p(u):
+            pT_ps = psum.tile([P, 2, USER], BF16, name="pT_ps", tag="flipped", bufs=1)
             for nb in range(2):
                 for jb in range(2):
                     nc.tensor.transpose(
-                        pT_ps[:, nb, jb * P : (jb + 1) * P], p_sb[:, jb, nb * P : (nb + 1) * P], ident_bf[:]
+                        pT_ps[:, nb, jb * P : (jb + 1) * P], p_of[u][:, jb, nb * P : (nb + 1) * P], ident_bf[:]
                     )
-            nc.vector.tensor_copy(pT_sb[:, u, :, :], pT_ps[:])
-            rcol = work.tile([P, 2], F32, name="rcol")
-            nc.vector.reciprocal(rcol[:], den[:])
-            spread = work.tile([P, 2, P], F32, name="spread")
-            nc.gpsimd.tensor_copy(spread[:], rcol[:].unsqueeze(2).to_broadcast([P, 2, P]))
-            r_ps = psum.tile([P, USER], F32, name="r_ps", tag="flipped")
-            for jb in range(2):
-                nc.tensor.transpose(r_ps[:, jb * P : (jb + 1) * P], spread[:, jb, :], ident_f[:])
-            nc.scalar.copy(rden_sb[:, tok : tok + USER], r_ps[:])
+            copy_out(pT_sb[:, u, :, :], pT_ps[:], u * USER // CHUNK)
 
-        def attend_and_place(c, half):
-            num_sb = held.tile([P, HALF], F32, name=f"num_sb{c}_{half}")
-            for pair in range(HALF // CHUNK):
-                num_ps = psum.tile([P, CHUNK], F32, name="num_ps")
-                for s in range(CHUNK // USER):
-                    u = (half * HALF + pair * CHUNK) // USER + s
-                    for nb in range(2):
-                        nc.tensor.matmul(
-                            num_ps[:, s * USER : (s + 1) * USER],
-                            vT_sb[:, 2 * u + nb, c * P : (c + 1) * P],
-                            pT_sb[:, u, nb, :],
-                            start=nb == 0,
-                            stop=nb == 1,
-                        )
-                nc.scalar.copy(num_sb[:, pair * CHUNK : (pair + 1) * CHUNK], num_ps[:])
+        def flip_r(u):
+            r_ps = psum.tile([P, USER], F32, name="r_ps", tag="flipped", bufs=1)
+            for jb in range(2):
+                nc.tensor.transpose(r_ps[:, jb * P : (jb + 1) * P], spread_of[u][:, jb, :], ident_f[:])
+            nc.scalar.copy(rden_sb[:, u * USER : (u + 1) * USER], r_ps[:])
+
+        def attend(c, t):
+            num_ps = psum.tile([P, CHUNK], F32, name="num_ps")
+            for s in range(CHUNK // USER):
+                u = t * (CHUNK // USER) + s
+                for nb in range(2):
+                    nc.tensor.matmul(
+                        num_ps[:, s * USER : (s + 1) * USER],
+                        vT_sb[:, 2 * u + nb, c * P : (c + 1) * P],
+                        pT_sb[:, u, nb, :],
+                        start=nb == 0,
+                        stop=nb == 1,
+                    )
+            col = t * CHUNK % HALF
+            nc.scalar.copy(num_sb[c][t * CHUNK // HALF][:, col : col + CHUNK], num_ps[:])
+
+        def place(c, half):
             nc.vector.tensor_tensor(
                 window[c][:].indirect(offsets[:, half * (HALF // 16) : (half + 1) * (HALF // 16)]),
-                num_sb[:],
+                num_sb[c][half][:],
                 rden_sb[:, half * HALF : (half + 1) * HALF],
                 ALU.mult,
             )
 
+        in_turn(hidden_layer(0, 0), hidden_layer(1, 0))
         for half in range(TOKENS // HALF):
-            chunks = [half * (HALF // CHUNK) + s for s in range(HALF // CHUNK)]
-            for t in chunks:
-                h_q = project_h(0, t)
-                h_k = project_h(1, t)
-                project_q(h_q, t)
-                project_k(h_k, t, half)
-            for t in chunks:
-                project_v(project_h(2, t), t)
-            for u in range(half * (HALF // USER), (half + 1) * (HALF // USER)):
-                softmax(u)
-            for c in range(DB):
-                attend_and_place(c, half)
-                if half == TOKENS // HALF - 1:
-                    nc.sync.dma_start(out[c * P : (c + 1) * P, :], window[c][:])
+            t0, t1 = 2 * half, 2 * half + 1
+            u = 4 * half
+            late = []
+            if half > 0:
+                late = [(attend, c, t0 - 1) for c in range(DB)]
+            in_turn(
+                project(q_block, t0),
+                hidden_layer(0, t1),
+                late,
+                [(place, c, half - 1) for c in range(DB - 1) if half > 0],
+            )
+            in_turn(project(k_block, t0), hidden_layer(1, t1))
+            in_turn(project(q_block, t1), hidden_layer(2, t0), [None, (scores, u), (scores, u + 1)])
+            in_turn(
+                project(k_block, t1),
+                hidden_layer(2, t1),
+                [(weights, u), (weights, u + 1), (flip_p, u + 1), (flip_r, u)],
+                [None, (flip_p, u), None, (flip_r, u + 1)],
+                [None, (place, DB - 1, half - 1) if half > 0 else None],
+            )
+            in_turn(
+                project(v_block, t0),
+                hidden_layer(0, t0 + 2),
+                [(scores, u + 2), (scores, u + 3), None, (flip_p, u + 2)],
+                [(weights, u + 2), (weights, u + 3)],
+            )
+            in_turn(
+                project(v_block, t1),
+                hidden_layer(1, t0 + 2),
+                [(flip_p, u + 3), (flip_r, u + 2), (flip_r, u + 3)],
+                [(attend, c, t0) for c in range(DB)],
+            )
+        last = TOKENS // HALF - 1
+        for c in range(DB):
+            attend(c, TOKENS // CHUNK - 1)
+            place(c, last)
+            nc.sync.dma_start(out[c * P : (c + 1) * P, :], window[c][:])

@@ -17,16 +17,11 @@ SLOTS = 4096
 USER = 256
 CHUNK = 512
 HALF = 1024
+SIDE = 256
+PSUM_BANKS = 8
 SCALE = 1.0 / math.sqrt(D)
 
 FLOPS = 2 * (STREAMS * P * D * TOKENS + STREAMS * D * D * TOKENS + 2 * TOKENS * USER * D)
-
-
-def in_turn(*queues):
-    for i in range(max(len(queue) for queue in queues)):
-        for queue in queues:
-            if i < len(queue) and queue[i] is not None:
-                queue[i][0](*queue[i][1:])
 
 
 def tile_nrmsmodel_b_kernel(tc, x, w_u, b_u, wq, bq, wk, wv, bv, base, offs, out):
@@ -34,9 +29,12 @@ def tile_nrmsmodel_b_kernel(tc, x, w_u, b_u, wq, bq, wk, wv, bv, base, offs, out
     with (
         tc.tile_pool(name="held", bufs=1) as held,
         tc.tile_pool(name="hidden", bufs=6) as hidden,
-        tc.tile_pool(name="work", bufs=3) as work,
-        tc.psum_pool(name="psum", bufs=2) as psum,
+        tc.tile_pool(name="work", bufs=4) as work,
+        tc.psum_pool(name="psum", bufs=PSUM_BANKS) as psum,
     ):
+        def bank(shape, dtype):
+            return psum.tile(shape, dtype, name="bank")
+
         offsets = held.tile([P, TOKENS // 16], U16, name="offsets")
         nc.sync.dma_start(offsets[:], offs)
 
@@ -92,163 +90,139 @@ def tile_nrmsmodel_b_kernel(tc, x, w_u, b_u, wq, bq, wk, wv, bv, base, offs, out
         vT_sb = held.tile([P, TOKENS // P, D], BF16, name="vT_sb")
         pT_sb = held.tile([P, TOKENS // USER, 2, USER], BF16, name="pT_sb")
         rden_sb = held.tile([P, TOKENS], F32, name="rden_sb")
-        num_sb = [
-            [held.tile([P, HALF], F32, name=f"num_sb{c}_{half}") for half in range(TOKENS // HALF)] for c in range(DB)
-        ]
 
-        def copy_out(dst, src, t):
-            if t * CHUNK < HALF:
-                nc.vector.tensor_copy(dst, src)
-            else:
-                nc.scalar.copy(dst, src)
+        def project_h(i, t):
+            h = hidden.tile([P, DB, CHUNK], BF16, name="h")
+            for b in range(DB):
+                acc = bank([P, CHUNK], F32)
+                nc.tensor.matmul(acc[:], w_u_blocks[:, b, :], x_sb[i][:, t * CHUNK : (t + 1) * CHUNK])
+                nc.scalar.activation(h[:, b, :], acc[:], ACT.Identity, bias=b_u_sb[:, b : b + 1])
+            return h
 
-        h_of = {}
+        def project_q(h, t):
+            for b in range(DB):
+                acc = bank([P, CHUNK], F32)
+                for kb in range(DB):
+                    nc.tensor.matmul(acc[:], wq_blocks[:, kb, b, :], h[:, kb, :], start=kb == 0, stop=kb == DB - 1)
+                nc.scalar.activation(
+                    q_sb[:, b, t * CHUNK : (t + 1) * CHUNK], acc[:], ACT.Identity, bias=bq_sb[:, b : b + 1]
+                )
 
-        def hidden_block(i, t, b):
-            acc = psum.tile([P, CHUNK], F32, name="acc", bufs=3)
-            nc.tensor.matmul(acc[:], w_u_blocks[:, b, :], x_sb[i][:, t * CHUNK : (t + 1) * CHUNK])
-            if t * CHUNK < HALF and b % 2 == 1:
-                nc.vector.tensor_scalar_add(h_of[i, t][:, b, :], acc[:], b_u_sb[:, b : b + 1])
-            else:
-                nc.scalar.activation(h_of[i, t][:, b, :], acc[:], ACT.Identity, bias=b_u_sb[:, b : b + 1])
+        def project_k(h, t):
+            for b in range(DB):
+                acc = bank([P, CHUNK], F32)
+                for kb in range(DB):
+                    nc.tensor.matmul(acc[:], wk_blocks[:, kb, b, :], h[:, kb, :], start=kb == 0, stop=kb == DB - 1)
+                nc.scalar.copy(k_sb[:, b, t * CHUNK : (t + 1) * CHUNK], acc[:])
 
-        def hidden_layer(i, t):
-            if t * CHUNK >= TOKENS:
-                return []
-            h_of[i, t] = hidden.tile([P, DB, CHUNK], BF16, name="h")
-            return [(hidden_block, i, t, b) for b in range(DB)]
+        def project_v(h_v, half, side):
+            cols = slice(side * SIDE, (side + 1) * SIDE)
+            bias = bv_sb[:, cols].unsqueeze(1).to_broadcast([P, 2, SIDE])
+            for pair in range(HALF // (2 * P)):
+                acc = bank([P, 2, SIDE], F32)
+                for s in range(2):
+                    tok = (2 * pair + s) * P
+                    h = h_v[tok // CHUNK]
+                    for kb in range(DB):
+                        nc.tensor.matmul(
+                            acc[:, s, :],
+                            h[:, kb, tok % CHUNK : tok % CHUNK + P],
+                            wv_sb[:, kb, cols],
+                            start=kb == 0,
+                            stop=kb == DB - 1,
+                        )
+                block = half * (HALF // P) + 2 * pair
+                v_out = vT_sb[:, block : block + 2, cols]
+                if side == 0:
+                    nc.vector.tensor_tensor(v_out, acc[:], bias, ALU.add)
+                else:
+                    v_raw = work.tile([P, 2, SIDE], F32, name="v_raw", bufs=2)
+                    nc.scalar.copy(v_raw[:], acc[:])
+                    nc.gpsimd.tensor_tensor(v_out, v_raw[:], bias, ALU.add)
 
-        def q_block(t, b):
-            acc = psum.tile([P, CHUNK], F32, name="acc", bufs=3)
-            for kb in range(DB):
-                nc.tensor.matmul(acc[:], wq_blocks[:, kb, b, :], h_of[0, t][:, kb, :], start=kb == 0, stop=kb == DB - 1)
-            nc.scalar.activation(q_sb[:, b, t * CHUNK : (t + 1) * CHUNK], acc[:], ACT.Identity, bias=bq_sb[:, b : b + 1])
-
-        def k_block(t, b):
-            acc = psum.tile([P, CHUNK], F32, name="acc", bufs=3)
-            for kb in range(DB):
-                nc.tensor.matmul(acc[:], wk_blocks[:, kb, b, :], h_of[1, t][:, kb, :], start=kb == 0, stop=kb == DB - 1)
-            copy_out(k_sb[:, b, t * CHUNK : (t + 1) * CHUNK], acc[:], t)
-
-        def v_block(t, s):
-            acc = psum.tile([P, D], F32, name="acc", bufs=3)
-            for kb in range(DB):
-                nc.tensor.matmul(acc[:], h_of[2, t][:, kb, s * P : (s + 1) * P], wv_sb[:, kb, :], start=kb == 0, stop=kb == DB - 1)
-            nc.vector.tensor_tensor(vT_sb[:, t * (CHUNK // P) + s, :], acc[:], bv_sb[:], ALU.add)
-
-        def project(block, t):
-            return [(block, t, b) for b in range(DB)]
-
-        scores_of, shift_of, p_of, spread_of = {}, {}, {}, {}
-
-        def scores(u):
+        def softmax(u):
             tok = u * USER
-            scores_of[u] = psum.tile([P, 2, USER], F32, name="scores")
+            scores = bank([P, 2, USER], F32)
             for jb in range(2):
                 for b in range(DB):
                     nc.tensor.matmul(
-                        scores_of[u][:, jb, :],
+                        scores[:, jb, :],
                         q_sb[:, b, tok + jb * P : tok + (jb + 1) * P],
                         k_sb[:, b, tok : tok + USER],
                         start=b == 0,
                         stop=b == DB - 1,
                     )
             top = work.tile([P, 2], F32, name="top")
-            nc.vector.reduce_max(top[:], scores_of[u][:], axis=AXIS.X)
-            shift_of[u] = work.tile([P, 2], F32, name="shift")
-            nc.vector.tensor_scalar_mul(shift_of[u][:], top[:], -SCALE)
-
-        def weights(u):
-            p_of[u] = work.tile([P, 2, USER], BF16, name="p_sb")
+            nc.vector.reduce_max(top[:], scores[:], axis=AXIS.X)
+            shift = work.tile([P, 2], F32, name="shift")
+            nc.vector.tensor_scalar_mul(shift[:], top[:], -SCALE)
+            p_sb = work.tile([P, 2, USER], BF16, name="p_sb")
             den = work.tile([P, 2], F32, name="den")
             for jb in range(2):
                 nc.scalar.activation(
-                    p_of[u][:, jb, :],
-                    scores_of[u][:, jb, :],
+                    p_sb[:, jb, :],
+                    scores[:, jb, :],
                     ACT.Exp,
-                    bias=shift_of[u][:, jb : jb + 1],
+                    bias=shift[:, jb : jb + 1],
                     scale=SCALE,
                     accum_out=den[:, jb : jb + 1],
                 )
             rcol = work.tile([P, 2], F32, name="rcol")
             nc.vector.reciprocal(rcol[:], den[:])
-            spread_of[u] = work.tile([P, 2, P], F32, name="spread")
-            nc.gpsimd.tensor_copy(spread_of[u][:], rcol[:].unsqueeze(2).to_broadcast([P, 2, P]))
+            spread = work.tile([P, 2, P], F32, name="spread")
+            nc.gpsimd.tensor_copy(spread[:], rcol[:].unsqueeze(2).to_broadcast([P, 2, P]))
+            return p_sb, spread
 
-        def flip_p(u):
-            pT_ps = psum.tile([P, 2, USER], BF16, name="pT_ps", tag="flipped", bufs=1)
+        def flip(u, p_sb, spread):
+            pT_ps = bank([P, 2, USER], BF16)
             for nb in range(2):
                 for jb in range(2):
                     nc.tensor.transpose(
-                        pT_ps[:, nb, jb * P : (jb + 1) * P], p_of[u][:, jb, nb * P : (nb + 1) * P], ident_bf[:]
+                        pT_ps[:, nb, jb * P : (jb + 1) * P], p_sb[:, jb, nb * P : (nb + 1) * P], ident_bf[:]
                     )
-            copy_out(pT_sb[:, u, :, :], pT_ps[:], u * USER // CHUNK)
-
-        def flip_r(u):
-            r_ps = psum.tile([P, USER], F32, name="r_ps", tag="flipped", bufs=1)
+            nc.scalar.copy(pT_sb[:, u, :, :], pT_ps[:])
+            r_ps = bank([P, USER], F32)
             for jb in range(2):
-                nc.tensor.transpose(r_ps[:, jb * P : (jb + 1) * P], spread_of[u][:, jb, :], ident_f[:])
+                nc.tensor.transpose(r_ps[:, jb * P : (jb + 1) * P], spread[:, jb, :], ident_f[:])
             nc.scalar.copy(rden_sb[:, u * USER : (u + 1) * USER], r_ps[:])
 
-        def attend(c, t):
-            num_ps = psum.tile([P, CHUNK], F32, name="num_ps")
-            for s in range(CHUNK // USER):
-                u = t * (CHUNK // USER) + s
-                for nb in range(2):
-                    nc.tensor.matmul(
-                        num_ps[:, s * USER : (s + 1) * USER],
-                        vT_sb[:, 2 * u + nb, c * P : (c + 1) * P],
-                        pT_sb[:, u, nb, :],
-                        start=nb == 0,
-                        stop=nb == 1,
-                    )
-            col = t * CHUNK % HALF
-            nc.scalar.copy(num_sb[c][t * CHUNK // HALF][:, col : col + CHUNK], num_ps[:])
-
-        def place(c, half):
+        def attend_and_place(c, half):
+            num_sb = held.tile([P, HALF], F32, name=f"num_sb{c}_{half}")
+            for pair in range(HALF // CHUNK):
+                num_ps = bank([P, CHUNK], F32)
+                for s in range(CHUNK // USER):
+                    u = (half * HALF + pair * CHUNK) // USER + s
+                    for nb in range(2):
+                        nc.tensor.matmul(
+                            num_ps[:, s * USER : (s + 1) * USER],
+                            vT_sb[:, 2 * u + nb, c * P : (c + 1) * P],
+                            pT_sb[:, u, nb, :],
+                            start=nb == 0,
+                            stop=nb == 1,
+                        )
+                nc.scalar.copy(num_sb[:, pair * CHUNK : (pair + 1) * CHUNK], num_ps[:])
             nc.vector.tensor_tensor(
                 window[c][:].indirect(offsets[:, half * (HALF // 16) : (half + 1) * (HALF // 16)]),
-                num_sb[c][half][:],
+                num_sb[:],
                 rden_sb[:, half * HALF : (half + 1) * HALF],
                 ALU.mult,
             )
 
-        in_turn(hidden_layer(0, 0), hidden_layer(1, 0))
         for half in range(TOKENS // HALF):
-            t0, t1 = 2 * half, 2 * half + 1
-            u = 4 * half
-            late = []
-            if half > 0:
-                late = [(attend, c, t0 - 1) for c in range(DB)]
-            in_turn(
-                project(q_block, t0),
-                hidden_layer(0, t1),
-                late,
-                [(place, c, half - 1) for c in range(DB - 1) if half > 0],
-            )
-            in_turn(project(k_block, t0), hidden_layer(1, t1))
-            in_turn(project(q_block, t1), hidden_layer(2, t0), [None, (scores, u), (scores, u + 1)])
-            in_turn(
-                project(k_block, t1),
-                hidden_layer(2, t1),
-                [(weights, u), (weights, u + 1), (flip_p, u + 1), (flip_r, u)],
-                [None, (flip_p, u), None, (flip_r, u + 1)],
-                [None, (place, DB - 1, half - 1) if half > 0 else None],
-            )
-            in_turn(
-                project(v_block, t0),
-                hidden_layer(0, t0 + 2),
-                [(scores, u + 2), (scores, u + 3), None, (flip_p, u + 2)],
-                [(weights, u + 2), (weights, u + 3)],
-            )
-            in_turn(
-                project(v_block, t1),
-                hidden_layer(1, t0 + 2),
-                [(flip_p, u + 3), (flip_r, u + 2), (flip_r, u + 3)],
-                [(attend, c, t0) for c in range(DB)],
-            )
-        last = TOKENS // HALF - 1
-        for c in range(DB):
-            attend(c, TOKENS // CHUNK - 1)
-            place(c, last)
-            nc.sync.dma_start(out[c * P : (c + 1) * P, :], window[c][:])
+            chunks = [half * (HALF // CHUNK) + s for s in range(HALF // CHUNK)]
+            users = [half * (HALF // USER) + s for s in range(HALF // USER)]
+            for t in chunks:
+                h_q = project_h(0, t)
+                h_k = project_h(1, t)
+                project_q(h_q, t)
+                project_k(h_k, t)
+            h_v = [project_h(2, t) for t in chunks]
+            weights = [softmax(u) for u in users]
+            for u, (p_sb, spread) in zip(users, weights):
+                flip(u, p_sb, spread)
+            for side in range(D // SIDE):
+                project_v(h_v, half, side)
+                for c in range(side * (SIDE // P), (side + 1) * (SIDE // P)):
+                    attend_and_place(c, half)
+                    if half == TOKENS // HALF - 1:
+                        nc.sync.dma_start(out[c * P : (c + 1) * P, :], window[c][:])

@@ -122,23 +122,17 @@ def tile_nrmsmodel_b_kernel(tc, x, w_u, b_u, wq, bq, wk, wv, bv, base, offs, out
                 acc = bank([P, 2, SIDE], F32)
                 for s in range(2):
                     tok = (2 * pair + s) * P
-                    h = h_v[tok // CHUNK]
+                    h_t = h_v[tok // CHUNK]
                     for kb in range(DB):
                         nc.tensor.matmul(
                             acc[:, s, :],
-                            h[:, kb, tok % CHUNK : tok % CHUNK + P],
+                            h_t[:, kb, tok % CHUNK : tok % CHUNK + P],
                             wv_sb[:, kb, cols],
                             start=kb == 0,
                             stop=kb == DB - 1,
                         )
                 block = half * (HALF // P) + 2 * pair
-                v_out = vT_sb[:, block : block + 2, cols]
-                if side == 0:
-                    nc.vector.tensor_tensor(v_out, acc[:], bias, ALU.add)
-                else:
-                    v_raw = work.tile([P, 2, SIDE], F32, name="v_raw", bufs=2)
-                    nc.scalar.copy(v_raw[:], acc[:])
-                    nc.gpsimd.tensor_tensor(v_out, v_raw[:], bias, ALU.add)
+                nc.vector.tensor_tensor(vT_sb[:, block : block + 2, cols], acc[:], bias, ALU.add)
 
         def softmax(u):
             tok = u * USER
@@ -208,21 +202,31 @@ def tile_nrmsmodel_b_kernel(tc, x, w_u, b_u, wq, bq, wk, wv, bv, base, offs, out
                 ALU.mult,
             )
 
+        h = {(0, 0): project_h(0, 0), (1, 0): project_h(1, 0)}
         for half in range(TOKENS // HALF):
-            chunks = [half * (HALF // CHUNK) + s for s in range(HALF // CHUNK)]
+            last = half == TOKENS // HALF - 1
+            t0, t1 = 2 * half, 2 * half + 1
             users = [half * (HALF // USER) + s for s in range(HALF // USER)]
-            for t in chunks:
-                h_q = project_h(0, t)
-                h_k = project_h(1, t)
-                project_q(h_q, t)
-                project_k(h_k, t)
-            h_v = [project_h(2, t) for t in chunks]
+            project_q(h[0, t0], t0)
+            h[0, t1] = project_h(0, t1)
+            project_k(h[1, t0], t0)
+            h[1, t1] = project_h(1, t1)
+            project_q(h[0, t1], t1)
+            h[2, t0] = project_h(2, t0)
+            project_k(h[1, t1], t1)
+            h[2, t1] = project_h(2, t1)
             weights = [softmax(u) for u in users]
             for u, (p_sb, spread) in zip(users, weights):
                 flip(u, p_sb, spread)
-            for side in range(D // SIDE):
-                project_v(h_v, half, side)
-                for c in range(side * (SIDE // P), (side + 1) * (SIDE // P)):
-                    attend_and_place(c, half)
-                    if half == TOKENS // HALF - 1:
-                        nc.sync.dma_start(out[c * P : (c + 1) * P, :], window[c][:])
+            project_v([h[2, t0], h[2, t1]], half, 0)
+            if last:
+                attend_and_place(0, half)
+            else:
+                h[0, t0 + 2] = project_h(0, t0 + 2)
+            project_v([h[2, t0], h[2, t1]], half, 1)
+            if not last:
+                h[1, t0 + 2] = project_h(1, t0 + 2)
+            for c in range(1 if last else 0, DB):
+                attend_and_place(c, half)
+        for c in range(DB):
+            nc.sync.dma_start(out[c * P : (c + 1) * P, :], window[c][:])

@@ -91,12 +91,18 @@ def tile_nrmsmodel_b_kernel(tc, x, w_u, b_u, wq, bq, wk, wv, bv, base, offs, out
         pT_sb = held.tile([P, TOKENS // USER, 2, USER], BF16, name="pT_sb")
         rden_sb = held.tile([P, TOKENS], F32, name="rden_sb")
 
+        def vector_is_free(t):
+            return t * CHUNK < HALF
+
         def project_h(i, t):
             h = hidden.tile([P, DB, CHUNK], BF16, name="h")
             for b in range(DB):
                 acc = bank([P, CHUNK], F32)
                 nc.tensor.matmul(acc[:], w_u_blocks[:, b, :], x_sb[i][:, t * CHUNK : (t + 1) * CHUNK])
-                nc.scalar.activation(h[:, b, :], acc[:], ACT.Identity, bias=b_u_sb[:, b : b + 1])
+                if vector_is_free(t) and b % 2 == 1:
+                    nc.vector.tensor_scalar_add(h[:, b, :], acc[:], b_u_sb[:, b : b + 1])
+                else:
+                    nc.scalar.activation(h[:, b, :], acc[:], ACT.Identity, bias=b_u_sb[:, b : b + 1])
             return h
 
         def project_q(h, t):
@@ -113,7 +119,10 @@ def tile_nrmsmodel_b_kernel(tc, x, w_u, b_u, wq, bq, wk, wv, bv, base, offs, out
                 acc = bank([P, CHUNK], F32)
                 for kb in range(DB):
                     nc.tensor.matmul(acc[:], wk_blocks[:, kb, b, :], h[:, kb, :], start=kb == 0, stop=kb == DB - 1)
-                nc.scalar.copy(k_sb[:, b, t * CHUNK : (t + 1) * CHUNK], acc[:])
+                if vector_is_free(t):
+                    nc.vector.tensor_copy(k_sb[:, b, t * CHUNK : (t + 1) * CHUNK], acc[:])
+                else:
+                    nc.scalar.copy(k_sb[:, b, t * CHUNK : (t + 1) * CHUNK], acc[:])
 
         def project_v(h_v, half, side):
             cols = slice(side * SIDE, (side + 1) * SIDE)
@@ -174,11 +183,11 @@ def tile_nrmsmodel_b_kernel(tc, x, w_u, b_u, wq, bq, wk, wv, bv, base, offs, out
                     nc.tensor.transpose(
                         pT_ps[:, nb, jb * P : (jb + 1) * P], p_sb[:, jb, nb * P : (nb + 1) * P], ident_bf[:]
                     )
-            nc.scalar.copy(pT_sb[:, u, :, :], pT_ps[:])
+            nc.vector.tensor_copy(pT_sb[:, u, :, :], pT_ps[:])
             r_ps = bank([P, USER], F32)
             for jb in range(2):
                 nc.tensor.transpose(r_ps[:, jb * P : (jb + 1) * P], spread[:, jb, :], ident_f[:])
-            nc.scalar.copy(rden_sb[:, u * USER : (u + 1) * USER], r_ps[:])
+            nc.vector.tensor_copy(rden_sb[:, u * USER : (u + 1) * USER], r_ps[:])
 
         def attend_and_place(c, half):
             num_sb = held.tile([P, HALF], F32, name=f"num_sb{c}_{half}")

@@ -124,24 +124,17 @@ def tile_nrmsmodel_b_kernel(tc, x, w_u, b_u, wq, bq, wk, wv, bv, base, offs, out
                 else:
                     nc.scalar.copy(k_sb[:, b, t * CHUNK : (t + 1) * CHUNK], acc[:])
 
-        def project_v(h_v, half, side):
+        def project_v(h_t, u, side):
             cols = slice(side * SIDE, (side + 1) * SIDE)
+            acc = bank([P, 2, SIDE], F32)
+            for s in range(2):
+                tok = u * USER % CHUNK + s * P
+                for kb in range(DB):
+                    nc.tensor.matmul(
+                        acc[:, s, :], h_t[:, kb, tok : tok + P], wv_sb[:, kb, cols], start=kb == 0, stop=kb == DB - 1
+                    )
             bias = bv_sb[:, cols].unsqueeze(1).to_broadcast([P, 2, SIDE])
-            for pair in range(HALF // (2 * P)):
-                acc = bank([P, 2, SIDE], F32)
-                for s in range(2):
-                    tok = (2 * pair + s) * P
-                    h_t = h_v[tok // CHUNK]
-                    for kb in range(DB):
-                        nc.tensor.matmul(
-                            acc[:, s, :],
-                            h_t[:, kb, tok % CHUNK : tok % CHUNK + P],
-                            wv_sb[:, kb, cols],
-                            start=kb == 0,
-                            stop=kb == DB - 1,
-                        )
-                block = half * (HALF // P) + 2 * pair
-                nc.vector.tensor_tensor(vT_sb[:, block : block + 2, cols], acc[:], bias, ALU.add)
+            nc.vector.tensor_tensor(vT_sb[:, 2 * u : 2 * u + 2, cols], acc[:], bias, ALU.add)
 
         def softmax(u):
             tok = u * USER
@@ -226,13 +219,14 @@ def tile_nrmsmodel_b_kernel(tc, x, w_u, b_u, wq, bq, wk, wv, bv, base, offs, out
             h[2, t1] = project_h(2, t1)
             weights = [softmax(u) for u in users]
             for u, (p_sb, spread) in zip(users, weights):
+                project_v(h[2, u * USER // CHUNK], u, 0)
                 flip(u, p_sb, spread)
-            project_v([h[2, t0], h[2, t1]], half, 0)
             if last:
                 attend_and_place(0, half)
             else:
                 h[0, t0 + 2] = project_h(0, t0 + 2)
-            project_v([h[2, t0], h[2, t1]], half, 1)
+            for u in users:
+                project_v(h[2, u * USER // CHUNK], u, 1)
             if not last:
                 h[1, t0 + 2] = project_h(1, t0 + 2)
             for c in range(1 if last else 0, DB):

@@ -19,6 +19,7 @@ CHUNK = 512
 HALF = 1024
 SIDE = 256
 PSUM_BANKS = 8
+WARM_UP = 5
 SCALE = 1.0 / math.sqrt(D)
 
 FLOPS = 2 * (STREAMS * P * D * TOKENS + STREAMS * D * D * TOKENS + 2 * TOKENS * USER * D)
@@ -34,9 +35,6 @@ def tile_nrmsmodel_b_kernel(tc, x, w_u, b_u, wq, bq, wk, wv, bv, base, offs, out
     ):
         def bank(shape, dtype):
             return psum.tile(shape, dtype, name="bank")
-
-        offsets = held.tile([P, TOKENS // 16], U16, name="offsets")
-        nc.sync.dma_start(offsets[:], offs)
 
         w_u_sb = held.tile([P, D], BF16, name="w_u_sb")
         nc.sync.dma_start(w_u_sb[:], w_u)
@@ -66,6 +64,8 @@ def tile_nrmsmodel_b_kernel(tc, x, w_u, b_u, wq, bq, wk, wv, bv, base, offs, out
         wv_sb = load_weight(wv, "wv_sb")
         bv_sb = held.tile([P, D], F32, name="bv_sb")
         nc.sync.dma_start(bv_sb[:], bv.rearrange("c one -> (c one)").partition_broadcast(P))
+        offsets = held.tile([P, TOKENS // 16], U16, name="offsets")
+        nc.sync.dma_start(offsets[:], offs)
         for i in range(STREAMS):
             load_x(i, 1)
         window = [held.tile([P, SLOTS], F32, name=f"window{c}") for c in range(DB)]
@@ -75,6 +75,12 @@ def tile_nrmsmodel_b_kernel(tc, x, w_u, b_u, wq, bq, wk, wv, bv, base, offs, out
         warm = held.tile([P, 1], F32, name="warm")
         nc.vector.memset(warm[:], 0.0)
         nc.scalar.activation(warm[:], warm[:], ACT.Exp)
+
+        zeros = held.tile([P, CHUNK], BF16, name="zeros")
+        nc.vector.memset(zeros[:], 0.0)
+        unread = bank([P, CHUNK], F32)
+        for i in range(WARM_UP):
+            nc.tensor.matmul(unread[:], zeros[:, :P], zeros[:])
 
         ident_bf = held.tile([P, P], BF16, name="ident_bf")
         make_identity(nc, ident_bf[:])
@@ -91,18 +97,12 @@ def tile_nrmsmodel_b_kernel(tc, x, w_u, b_u, wq, bq, wk, wv, bv, base, offs, out
         pT_sb = held.tile([P, TOKENS // USER, 2, USER], BF16, name="pT_sb")
         rden_sb = held.tile([P, TOKENS], F32, name="rden_sb")
 
-        def vector_is_free(t):
-            return t * CHUNK < HALF
-
         def project_h(i, t):
             h = hidden.tile([P, DB, CHUNK], BF16, name="h")
             for b in range(DB):
                 acc = bank([P, CHUNK], F32)
                 nc.tensor.matmul(acc[:], w_u_blocks[:, b, :], x_sb[i][:, t * CHUNK : (t + 1) * CHUNK])
-                if vector_is_free(t) and b % 2 == 1:
-                    nc.vector.tensor_scalar_add(h[:, b, :], acc[:], b_u_sb[:, b : b + 1])
-                else:
-                    nc.scalar.activation(h[:, b, :], acc[:], ACT.Identity, bias=b_u_sb[:, b : b + 1])
+                nc.scalar.activation(h[:, b, :], acc[:], ACT.Identity, bias=b_u_sb[:, b : b + 1])
             return h
 
         def project_q(h, t):
@@ -119,10 +119,7 @@ def tile_nrmsmodel_b_kernel(tc, x, w_u, b_u, wq, bq, wk, wv, bv, base, offs, out
                 acc = bank([P, CHUNK], F32)
                 for kb in range(DB):
                     nc.tensor.matmul(acc[:], wk_blocks[:, kb, b, :], h[:, kb, :], start=kb == 0, stop=kb == DB - 1)
-                if vector_is_free(t):
-                    nc.vector.tensor_copy(k_sb[:, b, t * CHUNK : (t + 1) * CHUNK], acc[:])
-                else:
-                    nc.scalar.copy(k_sb[:, b, t * CHUNK : (t + 1) * CHUNK], acc[:])
+                nc.scalar.copy(k_sb[:, b, t * CHUNK : (t + 1) * CHUNK], acc[:])
 
         def project_v(h_t, u, side):
             cols = slice(side * SIDE, (side + 1) * SIDE)

@@ -16,8 +16,6 @@ DB = D // P
 SLOTS = 4096
 USER = 256
 CHUNK = 512
-HALF = 1024
-SIDE = 256
 PSUM_BANKS = 8
 WARM_UP = 5
 SCALE = 1.0 / math.sqrt(D)
@@ -31,6 +29,7 @@ def tile_nrmsmodel_b_kernel(tc, x, w_u, b_u, wq, bq, wk, wv, bv, base, offs, out
         tc.tile_pool(name="held", bufs=1) as held,
         tc.tile_pool(name="hidden", bufs=6) as hidden,
         tc.tile_pool(name="work", bufs=4) as work,
+        tc.tile_pool(name="placed", bufs=6) as placed,
         tc.psum_pool(name="psum", bufs=PSUM_BANKS) as psum,
     ):
         def bank(shape, dtype):
@@ -41,7 +40,7 @@ def tile_nrmsmodel_b_kernel(tc, x, w_u, b_u, wq, bq, wk, wv, bv, base, offs, out
         x_sb = [held.tile([P, TOKENS], BF16, name=f"x_sb{i}") for i in range(STREAMS)]
 
         def load_x(i, half):
-            cols = slice(half * HALF, (half + 1) * HALF)
+            cols = slice(half * TOKENS // 2, (half + 1) * TOKENS // 2)
             nc.sync.dma_start(x_sb[i][:, cols], x[i, :, cols])
 
         def load_bias(bias, name):
@@ -121,17 +120,13 @@ def tile_nrmsmodel_b_kernel(tc, x, w_u, b_u, wq, bq, wk, wv, bv, base, offs, out
                     nc.tensor.matmul(acc[:], wk_blocks[:, kb, b, :], h[:, kb, :], start=kb == 0, stop=kb == DB - 1)
                 nc.scalar.copy(k_sb[:, b, t * CHUNK : (t + 1) * CHUNK], acc[:])
 
-        def project_v(h_t, u, side):
-            cols = slice(side * SIDE, (side + 1) * SIDE)
-            acc = bank([P, 2, SIDE], F32)
-            for s in range(2):
-                tok = u * USER % CHUNK + s * P
-                for kb in range(DB):
-                    nc.tensor.matmul(
-                        acc[:, s, :], h_t[:, kb, tok : tok + P], wv_sb[:, kb, cols], start=kb == 0, stop=kb == DB - 1
-                    )
-            bias = bv_sb[:, cols].unsqueeze(1).to_broadcast([P, 2, SIDE])
-            nc.vector.tensor_tensor(vT_sb[:, 2 * u : 2 * u + 2, cols], acc[:], bias, ALU.add)
+        def project_v(h_t, t, s):
+            acc = bank([P, D], F32)
+            for kb in range(DB):
+                nc.tensor.matmul(
+                    acc[:], h_t[:, kb, s * P : (s + 1) * P], wv_sb[:, kb, :], start=kb == 0, stop=kb == DB - 1
+                )
+            nc.vector.tensor_tensor(vT_sb[:, t * (CHUNK // P) + s, :], acc[:], bv_sb[:], ALU.add)
 
         def softmax(u):
             tok = u * USER
@@ -179,54 +174,46 @@ def tile_nrmsmodel_b_kernel(tc, x, w_u, b_u, wq, bq, wk, wv, bv, base, offs, out
                 nc.tensor.transpose(r_ps[:, jb * P : (jb + 1) * P], spread[:, jb, :], ident_f[:])
             nc.vector.tensor_copy(rden_sb[:, u * USER : (u + 1) * USER], r_ps[:])
 
-        def attend_and_place(c, half):
-            num_sb = held.tile([P, HALF], F32, name=f"num_sb{c}_{half}")
-            for pair in range(HALF // CHUNK):
-                num_ps = bank([P, CHUNK], F32)
-                for s in range(CHUNK // USER):
-                    u = (half * HALF + pair * CHUNK) // USER + s
-                    for nb in range(2):
-                        nc.tensor.matmul(
-                            num_ps[:, s * USER : (s + 1) * USER],
-                            vT_sb[:, 2 * u + nb, c * P : (c + 1) * P],
-                            pT_sb[:, u, nb, :],
-                            start=nb == 0,
-                            stop=nb == 1,
-                        )
-                nc.scalar.copy(num_sb[:, pair * CHUNK : (pair + 1) * CHUNK], num_ps[:])
+        def attend_and_place(c, t):
+            num_ps = bank([P, CHUNK], F32)
+            for s in range(CHUNK // USER):
+                u = t * (CHUNK // USER) + s
+                for nb in range(2):
+                    nc.tensor.matmul(
+                        num_ps[:, s * USER : (s + 1) * USER],
+                        vT_sb[:, 2 * u + nb, c * P : (c + 1) * P],
+                        pT_sb[:, u, nb, :],
+                        start=nb == 0,
+                        stop=nb == 1,
+                    )
+            num_sb = placed.tile([P, CHUNK], F32, name="num_sb")
+            nc.scalar.copy(num_sb[:], num_ps[:])
             nc.vector.tensor_tensor(
-                window[c][:].indirect(offsets[:, half * (HALF // 16) : (half + 1) * (HALF // 16)]),
+                window[c][:].indirect(offsets[:, t * (CHUNK // 16) : (t + 1) * (CHUNK // 16)]),
                 num_sb[:],
-                rden_sb[:, half * HALF : (half + 1) * HALF],
+                rden_sb[:, t * CHUNK : (t + 1) * CHUNK],
                 ALU.mult,
             )
 
-        h = {(0, 0): project_h(0, 0), (1, 0): project_h(1, 0)}
-        for half in range(TOKENS // HALF):
-            last = half == TOKENS // HALF - 1
-            t0, t1 = 2 * half, 2 * half + 1
-            users = [half * (HALF // USER) + s for s in range(HALF // USER)]
-            project_q(h[0, t0], t0)
-            h[0, t1] = project_h(0, t1)
-            project_k(h[1, t0], t0)
-            h[1, t1] = project_h(1, t1)
-            project_q(h[0, t1], t1)
-            h[2, t0] = project_h(2, t0)
-            project_k(h[1, t1], t1)
-            h[2, t1] = project_h(2, t1)
+        chunks = TOKENS // CHUNK
+        h = {(i, 0): project_h(i, 0) for i in range(STREAMS)}
+        project_q(h[0, 0], 0)
+        project_k(h[1, 0], 0)
+        for t in range(chunks):
+            users = [t * (CHUNK // USER) + s for s in range(CHUNK // USER)]
             weights = [softmax(u) for u in users]
+            for s in range(CHUNK // P):
+                project_v(h[2, t], t, s)
             for u, (p_sb, spread) in zip(users, weights):
-                project_v(h[2, u * USER // CHUNK], u, 0)
                 flip(u, p_sb, spread)
-            if last:
-                attend_and_place(0, half)
-            else:
-                h[0, t0 + 2] = project_h(0, t0 + 2)
-            for u in users:
-                project_v(h[2, u * USER // CHUNK], u, 1)
-            if not last:
-                h[1, t0 + 2] = project_h(1, t0 + 2)
-            for c in range(1 if last else 0, DB):
-                attend_and_place(c, half)
-        for c in range(DB):
-            nc.sync.dma_start(out[c * P : (c + 1) * P, :], window[c][:])
+            if t + 1 < chunks:
+                h[0, t + 1] = project_h(0, t + 1)
+                h[1, t + 1] = project_h(1, t + 1)
+            for c in range(DB):
+                attend_and_place(c, t)
+                if t == chunks - 1:
+                    nc.sync.dma_start(out[c * P : (c + 1) * P, :], window[c][:])
+            if t + 1 < chunks:
+                project_q(h[0, t + 1], t + 1)
+                h[2, t + 1] = project_h(2, t + 1)
+                project_k(h[1, t + 1], t + 1)

@@ -120,13 +120,13 @@ def tile_nrmsmodel_b_kernel(tc, x, w_u, b_u, wq, bq, wk, wv, bv, base, offs, out
                     nc.tensor.matmul(acc[:], wk_blocks[:, kb, b, :], h[:, kb, :], start=kb == 0, stop=kb == DB - 1)
                 nc.scalar.copy(k_sb[:, b, t * CHUNK : (t + 1) * CHUNK], acc[:])
 
-        def project_v(h_t, t, s):
-            acc = bank([P, D], F32)
+        def project_v(h_t, t, s, cols):
+            acc = bank([P, cols.stop - cols.start], F32)
             for kb in range(DB):
                 nc.tensor.matmul(
-                    acc[:], h_t[:, kb, s * P : (s + 1) * P], wv_sb[:, kb, :], start=kb == 0, stop=kb == DB - 1
+                    acc[:], h_t[:, kb, s * P : (s + 1) * P], wv_sb[:, kb, cols], start=kb == 0, stop=kb == DB - 1
                 )
-            nc.vector.tensor_tensor(vT_sb[:, t * (CHUNK // P) + s, :], acc[:], bv_sb[:], ALU.add)
+            nc.vector.tensor_tensor(vT_sb[:, t * (CHUNK // P) + s, cols], acc[:], bv_sb[:, cols], ALU.add)
 
         def softmax(u):
             tok = u * USER
@@ -196,24 +196,35 @@ def tile_nrmsmodel_b_kernel(tc, x, w_u, b_u, wq, bq, wk, wv, bv, base, offs, out
             )
 
         chunks = TOKENS // CHUNK
+        blocks = range(CHUNK // P)
         h = {(i, 0): project_h(i, 0) for i in range(STREAMS)}
         project_q(h[0, 0], 0)
         project_k(h[1, 0], 0)
-        for t in range(chunks):
+        for t in range(chunks - 1):
             users = [t * (CHUNK // USER) + s for s in range(CHUNK // USER)]
             weights = [softmax(u) for u in users]
-            for s in range(CHUNK // P):
-                project_v(h[2, t], t, s)
+            for s in blocks:
+                project_v(h[2, t], t, s, slice(0, D))
             for u, (p_sb, spread) in zip(users, weights):
                 flip(u, p_sb, spread)
-            if t + 1 < chunks:
-                h[0, t + 1] = project_h(0, t + 1)
-                h[1, t + 1] = project_h(1, t + 1)
+            h[0, t + 1] = project_h(0, t + 1)
             for c in range(DB):
                 attend_and_place(c, t)
-                if t == chunks - 1:
-                    nc.sync.dma_start(out[c * P : (c + 1) * P, :], window[c][:])
-            if t + 1 < chunks:
-                project_q(h[0, t + 1], t + 1)
-                h[2, t + 1] = project_h(2, t + 1)
-                project_k(h[1, t + 1], t + 1)
+            h[1, t + 1] = project_h(1, t + 1)
+            project_q(h[0, t + 1], t + 1)
+            h[2, t + 1] = project_h(2, t + 1)
+            project_k(h[1, t + 1], t + 1)
+
+        t = chunks - 1
+        users = [t * (CHUNK // USER) + s for s in range(CHUNK // USER)]
+        weights = [softmax(u) for u in users]
+        for s in blocks:
+            project_v(h[2, t], t, s, slice(0, D // 2))
+        for u, (p_sb, spread) in zip(users, weights):
+            flip(u, p_sb, spread)
+        for c in range(DB):
+            if c == DB // 2:
+                for s in blocks:
+                    project_v(h[2, t], t, s, slice(D // 2, D))
+            attend_and_place(c, t)
+            nc.sync.dma_start(out[c * P : (c + 1) * P, :], window[c][:])

@@ -39,9 +39,10 @@ def tile_nrmsmodel_b_kernel(tc, x, w_u, b_u, wq, bq, wk, wv, bv, base, offs, out
         nc.sync.dma_start(w_u_sb[:], w_u)
         x_sb = [held.tile([P, TOKENS], BF16, name=f"x_sb{i}") for i in range(STREAMS)]
 
-        def load_x(i, half):
-            cols = slice(half * TOKENS // 2, (half + 1) * TOKENS // 2)
+        def load_x(i, cols):
             nc.sync.dma_start(x_sb[i][:, cols], x[i, :, cols])
+
+        first, rest = slice(0, CHUNK), slice(CHUNK, TOKENS)
 
         def load_bias(bias, name):
             tile = held.tile([P, DB], F32, name=name)
@@ -53,20 +54,20 @@ def tile_nrmsmodel_b_kernel(tc, x, w_u, b_u, wq, bq, wk, wv, bv, base, offs, out
             nc.sync.dma_start(tile[:], w.rearrange("(p kb) d -> p kb d", kb=DB))
             return tile
 
-        load_x(0, 0)
-        load_x(1, 0)
+        load_x(0, first)
+        load_x(1, first)
         b_u_sb = load_bias(b_u, "b_u_sb")
         wq_sb = load_weight(wq, "wq_sb")
         bq_sb = load_bias(bq, "bq_sb")
         wk_sb = load_weight(wk, "wk_sb")
-        load_x(2, 0)
+        load_x(2, first)
         wv_sb = load_weight(wv, "wv_sb")
         bv_sb = held.tile([P, D], F32, name="bv_sb")
         nc.sync.dma_start(bv_sb[:], bv.rearrange("c one -> (c one)").partition_broadcast(P))
         offsets = held.tile([P, TOKENS // 16], U16, name="offsets")
         nc.sync.dma_start(offsets[:], offs)
         for i in range(STREAMS):
-            load_x(i, 1)
+            load_x(i, rest)
         window = [held.tile([P, SLOTS], F32, name=f"window{c}") for c in range(DB)]
         for c in range(DB):
             nc.sync.dma_start(window[c][:], base[c * P : (c + 1) * P, :])
@@ -101,7 +102,10 @@ def tile_nrmsmodel_b_kernel(tc, x, w_u, b_u, wq, bq, wk, wv, bv, base, offs, out
             for b in range(DB):
                 acc = bank([P, CHUNK], F32)
                 nc.tensor.matmul(acc[:], w_u_blocks[:, b, :], x_sb[i][:, t * CHUNK : (t + 1) * CHUNK])
-                nc.scalar.activation(h[:, b, :], acc[:], ACT.Identity, bias=b_u_sb[:, b : b + 1])
+                if t == 0 and b % 2 == 1:
+                    nc.vector.tensor_scalar_add(h[:, b, :], acc[:], b_u_sb[:, b : b + 1])
+                else:
+                    nc.scalar.activation(h[:, b, :], acc[:], ACT.Identity, bias=b_u_sb[:, b : b + 1])
             return h
 
         def project_q(h, t):
@@ -175,19 +179,19 @@ def tile_nrmsmodel_b_kernel(tc, x, w_u, b_u, wq, bq, wk, wv, bv, base, offs, out
             nc.vector.tensor_copy(rden_sb[:, u * USER : (u + 1) * USER], r_ps[:])
 
         def attend_and_place(c, t):
-            num_ps = bank([P, CHUNK], F32)
+            num_sb = placed.tile([P, CHUNK], F32, name="num_sb")
             for s in range(CHUNK // USER):
                 u = t * (CHUNK // USER) + s
+                num_ps = bank([P, USER], F32)
                 for nb in range(2):
                     nc.tensor.matmul(
-                        num_ps[:, s * USER : (s + 1) * USER],
+                        num_ps[:],
                         vT_sb[:, 2 * u + nb, c * P : (c + 1) * P],
                         pT_sb[:, u, nb, :],
                         start=nb == 0,
                         stop=nb == 1,
                     )
-            num_sb = placed.tile([P, CHUNK], F32, name="num_sb")
-            nc.scalar.copy(num_sb[:], num_ps[:])
+                nc.scalar.copy(num_sb[:, s * USER : (s + 1) * USER], num_ps[:])
             nc.vector.tensor_tensor(
                 window[c][:].indirect(offsets[:, t * (CHUNK // 16) : (t + 1) * (CHUNK // 16)]),
                 num_sb[:],
@@ -197,8 +201,9 @@ def tile_nrmsmodel_b_kernel(tc, x, w_u, b_u, wq, bq, wk, wv, bv, base, offs, out
 
         chunks = TOKENS // CHUNK
         blocks = range(CHUNK // P)
-        h = {(i, 0): project_h(i, 0) for i in range(STREAMS)}
+        h = {(0, 0): project_h(0, 0), (1, 0): project_h(1, 0)}
         project_q(h[0, 0], 0)
+        h[2, 0] = project_h(2, 0)
         project_k(h[1, 0], 0)
         for t in range(chunks - 1):
             users = [t * (CHUNK // USER) + s for s in range(CHUNK // USER)]
@@ -223,7 +228,7 @@ def tile_nrmsmodel_b_kernel(tc, x, w_u, b_u, wq, bq, wk, wv, bv, base, offs, out
         for u, (p_sb, spread) in zip(users, weights):
             flip(u, p_sb, spread)
         for c in range(DB):
-            if c == DB // 2:
+            if c == 1:
                 for s in blocks:
                     project_v(h[2, t], t, s, slice(D // 2, D))
             attend_and_place(c, t)

@@ -162,7 +162,7 @@ def tile_nrmsmodel_b_kernel(tc, x, w_u, b_u, wq, bq, wk, wv, bv, base, offs, out
             rcol = work.tile([P, 2], F32, name="rcol")
             nc.vector.reciprocal(rcol[:], den[:])
             spread = work.tile([P, 2, P], F32, name="spread")
-            nc.gpsimd.tensor_copy(spread[:], rcol[:].unsqueeze(2).to_broadcast([P, 2, P]))
+            nc.scalar.copy(spread[:], rcol[:].unsqueeze(2).to_broadcast([P, 2, P]))
             return p_sb, spread
 
         def flip(u, p_sb, spread):

@@ -17,7 +17,6 @@ SLOTS = 4096
 USER = 256
 CHUNK = 512
 PSUM_BANKS = 8
-WARM_UP = 5
 SCALE = 1.0 / math.sqrt(D)
 
 FLOPS = 2 * (STREAMS * P * D * TOKENS + STREAMS * D * D * TOKENS + 2 * TOKENS * USER * D)
@@ -75,12 +74,6 @@ def tile_nrmsmodel_b_kernel(tc, x, w_u, b_u, wq, bq, wk, wv, bv, base, offs, out
         warm = held.tile([P, 1], F32, name="warm")
         nc.vector.memset(warm[:], 0.0)
         nc.scalar.activation(warm[:], warm[:], ACT.Exp)
-
-        zeros = held.tile([P, CHUNK], BF16, name="zeros")
-        nc.vector.memset(zeros[:], 0.0)
-        unread = bank([P, CHUNK], F32)
-        for i in range(WARM_UP):
-            nc.tensor.matmul(unread[:], zeros[:, :P], zeros[:])
 
         ident_bf = held.tile([P, P], BF16, name="ident_bf")
         make_identity(nc, ident_bf[:])

@@ -152,13 +152,9 @@ def tile_nrmsmodel_b_kernel(tc, x, w_u, b_u, wq, bq, wk, wv, bv, base, offs, out
                     scale=SCALE,
                     accum_out=den[:, jb : jb + 1],
                 )
-            rcol = work.tile([P, 2], F32, name="rcol")
-            nc.vector.reciprocal(rcol[:], den[:])
-            spread = work.tile([P, 2, P], F32, name="spread")
-            nc.scalar.copy(spread[:], rcol[:].unsqueeze(2).to_broadcast([P, 2, P]))
-            return p_sb, spread
+            return p_sb, den
 
-        def flip(u, p_sb, spread):
+        def flip_p(u, p_sb):
             pT_ps = bank([P, 2, USER], BF16)
             for nb in range(2):
                 for jb in range(2):
@@ -166,10 +162,22 @@ def tile_nrmsmodel_b_kernel(tc, x, w_u, b_u, wq, bq, wk, wv, bv, base, offs, out
                         pT_ps[:, nb, jb * P : (jb + 1) * P], p_sb[:, jb, nb * P : (nb + 1) * P], ident_bf[:]
                     )
             nc.vector.tensor_copy(pT_sb[:, u, :, :], pT_ps[:])
+
+        def flip_r(u, den):
+            rcol = work.tile([P, 2], F32, name="rcol")
+            nc.vector.reciprocal(rcol[:], den[:])
+            spread = work.tile([P, 2, P], F32, name="spread")
+            nc.scalar.copy(spread[:], rcol[:].unsqueeze(2).to_broadcast([P, 2, P]))
             r_ps = bank([P, USER], F32)
             for jb in range(2):
                 nc.tensor.transpose(r_ps[:, jb * P : (jb + 1) * P], spread[:, jb, :], ident_f[:])
             nc.vector.tensor_copy(rden_sb[:, u * USER : (u + 1) * USER], r_ps[:])
+
+        def flip(users, weights):
+            for u, (p_sb, den) in zip(users, weights):
+                flip_p(u, p_sb)
+            for u, (p_sb, den) in zip(users, weights):
+                flip_r(u, den)
 
         def attend_and_place(c, t):
             num_sb = placed.tile([P, CHUNK], F32, name="num_sb")
@@ -203,8 +211,7 @@ def tile_nrmsmodel_b_kernel(tc, x, w_u, b_u, wq, bq, wk, wv, bv, base, offs, out
             weights = [softmax(u) for u in users]
             for s in blocks:
                 project_v(h[2, t], t, s, slice(0, D))
-            for u, (p_sb, spread) in zip(users, weights):
-                flip(u, p_sb, spread)
+            flip(users, weights)
             h[0, t + 1] = project_h(0, t + 1)
             for c in range(DB):
                 attend_and_place(c, t)
@@ -218,8 +225,7 @@ def tile_nrmsmodel_b_kernel(tc, x, w_u, b_u, wq, bq, wk, wv, bv, base, offs, out
         weights = [softmax(u) for u in users]
         for s in blocks:
             project_v(h[2, t], t, s, slice(0, D // 2))
-        for u, (p_sb, spread) in zip(users, weights):
-            flip(u, p_sb, spread)
+        flip(users, weights)
         for c in range(DB):
             if c == 1:
                 for s in blocks:

@@ -68,6 +68,18 @@ def tile_nrmsmodel_b_kernel(tc, x, w_u, b_u, wq, bq, wk, wv, bv, base, offs, out
         for i in range(STREAMS):
             load_x(i, rest)
         window = [held.tile([P, SLOTS], F32, name=f"window{c}") for c in range(DB)]
+
+        bv_terms = held.tile([P, D], BF16, name="bv_terms")
+        bv_left = held.tile([P, D], F32, name="bv_left")
+        shares = held.tile([P, P], BF16, name="shares")
+        nc.gpsimd.memset(shares[0:64, :], 1.0 / 32)
+        nc.gpsimd.memset(shares[64:P, :], 1.0 / 64)
+        nc.gpsimd.tensor_copy(bv_terms[:], bv_sb[:])
+        nc.gpsimd.tensor_tensor(bv_left[:], bv_sb[:], bv_terms[:], ALU.subtract)
+        nc.gpsimd.tensor_copy(bv_terms[32:64, :], bv_left[32:64, :])
+        nc.gpsimd.tensor_copy(bv_terms[64:P, :], bv_left[64:P, :])
+        nc.gpsimd.tensor_tensor(bv_left[64:P, :], bv_left[64:P, :], bv_terms[64:P, :], ALU.subtract)
+        nc.gpsimd.tensor_copy(bv_terms[64:P, :], bv_left[64:P, :])
         for c in range(DB):
             nc.sync.dma_start(window[c][:], base[c * P : (c + 1) * P, :])
 
@@ -124,6 +136,15 @@ def tile_nrmsmodel_b_kernel(tc, x, w_u, b_u, wq, bq, wk, wv, bv, base, offs, out
                     acc[:], h_t[:, kb, s * P : (s + 1) * P], wv_sb[:, kb, cols], start=kb == 0, stop=kb == DB - 1
                 )
             nc.vector.tensor_tensor(vT_sb[:, t * (CHUNK // P) + s, cols], acc[:], bv_sb[:, cols], ALU.add)
+
+        def project_v_late(h_t, t, s, cols):
+            acc = bank([P, cols.stop - cols.start], F32)
+            nc.tensor.matmul(acc[:], shares[:], bv_terms[:, cols], start=True, stop=False)
+            for kb in range(DB):
+                nc.tensor.matmul(
+                    acc[:], h_t[:, kb, s * P : (s + 1) * P], wv_sb[:, kb, cols], start=False, stop=kb == DB - 1
+                )
+            nc.scalar.copy(vT_sb[:, t * (CHUNK // P) + s, cols], acc[:])
 
         def softmax(u):
             tok = u * USER
@@ -210,25 +231,29 @@ def tile_nrmsmodel_b_kernel(tc, x, w_u, b_u, wq, bq, wk, wv, bv, base, offs, out
             users = [t * (CHUNK // USER) + s for s in range(CHUNK // USER)]
             weights = [softmax(u) for u in users]
             for s in blocks:
-                project_v(h[2, t], t, s, slice(0, D))
+                project_v(h[2, t], t, s, slice(0, D if t < chunks - 2 else D - P))
             flip(users, weights)
             h[0, t + 1] = project_h(0, t + 1)
-            for c in range(DB):
+            for c in range(DB if t < chunks - 2 else DB - 1):
                 attend_and_place(c, t)
             h[1, t + 1] = project_h(1, t + 1)
             project_q(h[0, t + 1], t + 1)
-            h[2, t + 1] = project_h(2, t + 1)
             project_k(h[1, t + 1], t + 1)
+            h[2, t + 1] = project_h(2, t + 1)
 
         t = chunks - 1
         users = [t * (CHUNK // USER) + s for s in range(CHUNK // USER)]
         weights = [softmax(u) for u in users]
         for s in blocks:
-            project_v(h[2, t], t, s, slice(0, D // 2))
+            project_v(h[2, t], t, s, slice(0, P))
         flip(users, weights)
         for c in range(DB):
-            if c == 1:
+            if c > 0:
                 for s in blocks:
-                    project_v(h[2, t], t, s, slice(D // 2, D))
+                    project_v_late(h[2, t], t, s, slice(c * P, (c + 1) * P))
+            if c == DB - 1:
+                for s in blocks:
+                    project_v_late(h[2, t - 1], t - 1, s, slice(D - P, D))
+                attend_and_place(c, t - 1)
             attend_and_place(c, t)
             nc.sync.dma_start(out[c * P : (c + 1) * P, :], window[c][:])

@@ -146,25 +146,26 @@ def tile_nrmsmodel_b_kernel(tc, x, w_u, b_u, wq, bq, wk, wv, bv, base, offs, out
                 )
             nc.scalar.copy(vT_sb[:, t * (CHUNK // P) + s, cols], acc[:])
 
-        def softmax(u):
-            tok = u * USER
-            scores = bank([P, 2, USER], F32)
-            for jb in range(2):
+        def softmax(tok, queries):
+            nj = queries // P
+            keys = slice(tok // USER * USER, (tok // USER + 1) * USER)
+            scores = bank([P, nj, USER], F32)
+            for jb in range(nj):
                 for b in range(DB):
                     nc.tensor.matmul(
                         scores[:, jb, :],
                         q_sb[:, b, tok + jb * P : tok + (jb + 1) * P],
-                        k_sb[:, b, tok : tok + USER],
+                        k_sb[:, b, keys],
                         start=b == 0,
                         stop=b == DB - 1,
                     )
-            top = work.tile([P, 2], F32, name="top")
+            top = work.tile([P, nj], F32, name="top")
             nc.vector.reduce_max(top[:], scores[:], axis=AXIS.X)
-            shift = work.tile([P, 2], F32, name="shift")
+            shift = work.tile([P, nj], F32, name="shift")
             nc.vector.tensor_scalar_mul(shift[:], top[:], -SCALE)
-            p_sb = work.tile([P, 2, USER], BF16, name="p_sb")
-            den = work.tile([P, 2], F32, name="den")
-            for jb in range(2):
+            p_sb = work.tile([P, nj, USER], BF16, name="p_sb")
+            den = work.tile([P, nj], F32, name="den")
+            for jb in range(nj):
                 nc.scalar.activation(
                     p_sb[:, jb, :],
                     scores[:, jb, :],
@@ -173,32 +174,34 @@ def tile_nrmsmodel_b_kernel(tc, x, w_u, b_u, wq, bq, wk, wv, bv, base, offs, out
                     scale=SCALE,
                     accum_out=den[:, jb : jb + 1],
                 )
-            return p_sb, den
+            return tok, p_sb, den
 
-        def flip_p(u, p_sb):
-            pT_ps = bank([P, 2, USER], BF16)
+        def flip_p(tok, p_sb):
+            u, j, queries = tok // USER, tok % USER, p_sb.shape[1] * P
+            pT_ps = bank([P, 2, queries], BF16)
             for nb in range(2):
-                for jb in range(2):
+                for jb in range(queries // P):
                     nc.tensor.transpose(
                         pT_ps[:, nb, jb * P : (jb + 1) * P], p_sb[:, jb, nb * P : (nb + 1) * P], ident_bf[:]
                     )
-            nc.vector.tensor_copy(pT_sb[:, u, :, :], pT_ps[:])
+            nc.vector.tensor_copy(pT_sb[:, u, :, j : j + queries], pT_ps[:])
 
-        def flip_r(u, den):
-            rcol = work.tile([P, 2], F32, name="rcol")
+        def flip_r(tok, den):
+            nj = den.shape[1]
+            rcol = work.tile([P, nj], F32, name="rcol")
             nc.vector.reciprocal(rcol[:], den[:])
-            spread = work.tile([P, 2, P], F32, name="spread")
-            nc.scalar.copy(spread[:], rcol[:].unsqueeze(2).to_broadcast([P, 2, P]))
-            r_ps = bank([P, USER], F32)
-            for jb in range(2):
-                nc.tensor.transpose(r_ps[:, jb * P : (jb + 1) * P], spread[:, jb, :], ident_f[:])
-            nc.vector.tensor_copy(rden_sb[:, u * USER : (u + 1) * USER], r_ps[:])
+            r_ps = bank([P, nj * P], F32)
+            for jb in range(nj):
+                nc.tensor.transpose(
+                    r_ps[:, jb * P : (jb + 1) * P], rcol[:, jb : jb + 1].to_broadcast([P, P]), ident_f[:]
+                )
+            nc.vector.tensor_copy(rden_sb[:, tok : tok + nj * P], r_ps[:])
 
-        def flip(users, weights):
-            for u, (p_sb, den) in zip(users, weights):
-                flip_p(u, p_sb)
-            for u, (p_sb, den) in zip(users, weights):
-                flip_r(u, den)
+        def flip(weights):
+            for tok, p_sb, den in weights:
+                flip_p(tok, p_sb)
+            for tok, p_sb, den in weights:
+                flip_r(tok, den)
 
         def attend_and_place(c, t):
             num_sb = placed.tile([P, CHUNK], F32, name="num_sb")
@@ -228,11 +231,10 @@ def tile_nrmsmodel_b_kernel(tc, x, w_u, b_u, wq, bq, wk, wv, bv, base, offs, out
         h[2, 0] = project_h(2, 0)
         project_k(h[1, 0], 0)
         for t in range(chunks - 1):
-            users = [t * (CHUNK // USER) + s for s in range(CHUNK // USER)]
-            weights = [softmax(u) for u in users]
+            weights = [softmax(t * CHUNK + s * USER, USER) for s in range(CHUNK // USER)]
             for s in blocks:
                 project_v(h[2, t], t, s, slice(0, D if t < chunks - 2 else D - P))
-            flip(users, weights)
+            flip(weights)
             h[0, t + 1] = project_h(0, t + 1)
             for c in range(DB if t < chunks - 2 else DB - 1):
                 attend_and_place(c, t)
@@ -242,11 +244,11 @@ def tile_nrmsmodel_b_kernel(tc, x, w_u, b_u, wq, bq, wk, wv, bv, base, offs, out
             h[2, t + 1] = project_h(2, t + 1)
 
         t = chunks - 1
-        users = [t * (CHUNK // USER) + s for s in range(CHUNK // USER)]
-        weights = [softmax(u) for u in users]
+        last_user = TOKENS - USER
+        weights = [softmax(t * CHUNK, USER), softmax(last_user, P), softmax(last_user + P, P)]
         for s in blocks:
             project_v(h[2, t], t, s, slice(0, P))
-        flip(users, weights)
+        flip(weights)
         for c in range(DB):
             if c > 0:
                 for s in blocks:

@@ -35,7 +35,7 @@ def tile_nrmsmodel_b_kernel(tc, x, w_u, b_u, wq, bq, wk, wv, bv, base, offs, out
             return psum.tile(shape, dtype, name="bank")
 
         w_u_sb = held.tile([P, D], BF16, name="w_u_sb")
-        nc.sync.dma_start(w_u_sb[:], w_u)
+        nc.scalar.dma_start(w_u_sb[:], w_u)
         x_sb = [held.tile([P, TOKENS], BF16, name=f"x_sb{i}") for i in range(STREAMS)]
 
         def load_x(i, cols):
@@ -203,10 +203,12 @@ def tile_nrmsmodel_b_kernel(tc, x, w_u, b_u, wq, bq, wk, wv, bv, base, offs, out
             for tok, p_sb, den in weights:
                 flip_r(tok, den)
 
-        def attend_and_place(c, t):
-            num_sb = placed.tile([P, CHUNK], F32, name="num_sb")
-            for s in range(CHUNK // USER):
-                u = t * (CHUNK // USER) + s
+        def attend_and_place(c, first_chunk, chunks=1):
+            tokens = chunks * CHUNK
+            tok = first_chunk * CHUNK
+            num_sb = placed.tile([P, tokens], F32, name=f"num_sb{chunks}")
+            for s in range(tokens // USER):
+                u = tok // USER + s
                 num_ps = bank([P, USER], F32)
                 for nb in range(2):
                     nc.tensor.matmul(
@@ -218,9 +220,9 @@ def tile_nrmsmodel_b_kernel(tc, x, w_u, b_u, wq, bq, wk, wv, bv, base, offs, out
                     )
                 nc.scalar.copy(num_sb[:, s * USER : (s + 1) * USER], num_ps[:])
             nc.vector.tensor_tensor(
-                window[c][:].indirect(offsets[:, t * (CHUNK // 16) : (t + 1) * (CHUNK // 16)]),
+                window[c][:].indirect(offsets[:, tok // 16 : (tok + tokens) // 16]),
                 num_sb[:],
-                rden_sb[:, t * CHUNK : (t + 1) * CHUNK],
+                rden_sb[:, tok : tok + tokens],
                 ALU.mult,
             )
 
@@ -256,6 +258,7 @@ def tile_nrmsmodel_b_kernel(tc, x, w_u, b_u, wq, bq, wk, wv, bv, base, offs, out
             if c == DB - 1:
                 for s in blocks:
                     project_v_late(h[2, t - 1], t - 1, s, slice(D - P, D))
-                attend_and_place(c, t - 1)
-            attend_and_place(c, t)
+                attend_and_place(c, t - 1, chunks=2)
+            else:
+                attend_and_place(c, t)
             nc.sync.dma_start(out[c * P : (c + 1) * P, :], window[c][:])

@@ -246,15 +246,17 @@ def tile_nrmsmodel_b_kernel(tc, x, w_u, b_u, wq, bq, wk, wv, bv, base, offs, out
             h[2, t + 1] = project_h(2, t + 1)
 
         t = chunks - 1
-        last_user = TOKENS - USER
-        weights = [softmax(t * CHUNK, USER), softmax(last_user, P), softmax(last_user + P, P)]
+        weights = [softmax(tok, P) for tok in range(t * CHUNK, TOKENS, P)]
         for s in blocks:
             project_v(h[2, t], t, s, slice(0, P))
         flip(weights)
         for c in range(DB):
-            if c > 0:
+            if c == 1:
                 for s in blocks:
-                    project_v_late(h[2, t], t, s, slice(c * P, (c + 1) * P))
+                    project_v_late(h[2, t], t, s, slice(P, 2 * P))
+            if c == 2:
+                for s in blocks:
+                    project_v_late(h[2, t], t, s, slice(2 * P, D))
             if c == DB - 1:
                 for s in blocks:
                     project_v_late(h[2, t - 1], t - 1, s, slice(D - P, D))

import math

import concourse.mybir as mybir
from concourse.masks import make_identity

BF16, F32, U16 = mybir.dt.bfloat16, mybir.dt.float32, mybir.dt.uint16
ACT = mybir.ActivationFunctionType
ALU = mybir.AluOpType
AXIS = mybir.AxisListType

P = 128
STREAMS = 3
TOKENS = 2048
D = 512
DB = D // P
SLOTS = 4096
USER = 256
CHUNK = 512
PSUM_BANKS = 8
SCALE = 1.0 / math.sqrt(D)

FLOPS = 2 * (STREAMS * P * D * TOKENS + STREAMS * D * D * TOKENS + 2 * TOKENS * USER * D)


def tile_nrmsmodel_b_kernel(tc, x, w_u, b_u, wq, bq, wk, wv, bv, base, offs, out):
    nc = tc.nc
    with (
        tc.tile_pool(name="held", bufs=1) as held,
        tc.tile_pool(name="hidden", bufs=6) as hidden,
        tc.tile_pool(name="work", bufs=4) as work,
        tc.tile_pool(name="placed", bufs=6) as placed,
        tc.psum_pool(name="psum", bufs=PSUM_BANKS) as psum,
    ):
        def bank(shape, dtype):
            return psum.tile(shape, dtype, name="bank")

        w_u_sb = held.tile([P, D], BF16, name="w_u_sb")
        nc.scalar.dma_start(w_u_sb[:], w_u)
        x_sb = [held.tile([P, TOKENS], BF16, name=f"x_sb{i}") for i in range(STREAMS)]

        def load_x(i, cols):
            nc.sync.dma_start(x_sb[i][:, cols], x[i, :, cols])

        first, rest = slice(0, CHUNK), slice(CHUNK, TOKENS)

        def load_bias(bias, name):
            tile = held.tile([P, DB], F32, name=name)
            nc.sync.dma_start(tile[:], bias.rearrange("(p b) one -> p (b one)", b=DB))
            return tile

        def load_weight(w, name):
            tile = held.tile([P, DB, D], BF16, name=name)
            nc.sync.dma_start(tile[:], w.rearrange("(p kb) d -> p kb d", kb=DB))
            return tile

        load_x(0, first)
        load_x(1, first)
        b_u_sb = load_bias(b_u, "b_u_sb")
        wq_sb = load_weight(wq, "wq_sb")
        bq_sb = load_bias(bq, "bq_sb")
        wk_sb = load_weight(wk, "wk_sb")
        load_x(2, first)
        wv_sb = load_weight(wv, "wv_sb")
        bv_sb = held.tile([P, D], F32, name="bv_sb")
        nc.sync.dma_start(bv_sb[:], bv.rearrange("c one -> (c one)").partition_broadcast(P))
        offsets = held.tile([P, TOKENS // 16], U16, name="offsets")
        nc.sync.dma_start(offsets[:], offs)
        for i in range(STREAMS):
            load_x(i, rest)
        window = [held.tile([P, SLOTS], F32, name=f"window{c}") for c in range(DB)]

        bv_terms = held.tile([P, D], BF16, name="bv_terms")
        bv_left = held.tile([P, D], F32, name="bv_left")
        shares = held.tile([P, P], BF16, name="shares")
        nc.gpsimd.memset(shares[0:64, :], 1.0 / 32)
        nc.gpsimd.memset(shares[64:P, :], 1.0 / 64)
        nc.gpsimd.tensor_copy(bv_terms[:], bv_sb[:])
        nc.gpsimd.tensor_tensor(bv_left[:], bv_sb[:], bv_terms[:], ALU.subtract)
        nc.gpsimd.tensor_copy(bv_terms[32:64, :], bv_left[32:64, :])
        nc.gpsimd.tensor_copy(bv_terms[64:P, :], bv_left[64:P, :])
        nc.gpsimd.tensor_tensor(bv_left[64:P, :], bv_left[64:P, :], bv_terms[64:P, :], ALU.subtract)
        nc.gpsimd.tensor_copy(bv_terms[64:P, :], bv_left[64:P, :])
        for c in range(DB):
            nc.sync.dma_start(window[c][:], base[c * P : (c + 1) * P, :])

        warm = held.tile([P, 1], F32, name="warm")
        nc.vector.memset(warm[:], 0.0)
        nc.scalar.activation(warm[:], warm[:], ACT.Exp)

        ident_bf = held.tile([P, P], BF16, name="ident_bf")
        make_identity(nc, ident_bf[:])
        ident_f = held.tile([P, P], F32, name="ident_f")
        make_identity(nc, ident_f[:])

        w_u_blocks = w_u_sb[:].rearrange("f (p b) -> f b p", b=DB)
        wq_blocks = wq_sb[:].rearrange("a kb (p b) -> a kb b p", b=DB)
        wk_blocks = wk_sb[:].rearrange("a kb (p b) -> a kb b p", b=DB)

        q_sb = held.tile([P, DB, TOKENS], BF16, name="q_sb")
        k_sb = held.tile([P, DB, TOKENS], BF16, name="k_sb")
        vT_sb = held.tile([P, TOKENS // P, D], BF16, name="vT_sb")
        pT_sb = held.tile([P, TOKENS // USER, 2, USER], BF16, name="pT_sb")
        rden_sb = held.tile([P, TOKENS], F32, name="rden_sb")

        def project_h(i, t):
            h = hidden.tile([P, DB, CHUNK], BF16, name="h")
            for b in range(DB):
                acc = bank([P, CHUNK], F32)
                nc.tensor.matmul(acc[:], w_u_blocks[:, b, :], x_sb[i][:, t * CHUNK : (t + 1) * CHUNK])
                if t == 0 and b % 2 == 1:
                    nc.vector.tensor_scalar_add(h[:, b, :], acc[:], b_u_sb[:, b : b + 1])
                else:
                    nc.scalar.activation(h[:, b, :], acc[:], ACT.Identity, bias=b_u_sb[:, b : b + 1])
            return h

        def project_q(h, t):
            for b in range(DB):
                acc = bank([P, CHUNK], F32)
                for kb in range(DB):
                    nc.tensor.matmul(acc[:], wq_blocks[:, kb, b, :], h[:, kb, :], start=kb == 0, stop=kb == DB - 1)
                nc.scalar.activation(
                    q_sb[:, b, t * CHUNK : (t + 1) * CHUNK], acc[:], ACT.Identity, bias=bq_sb[:, b : b + 1]
                )

        def project_k(h, t):
            for b in range(DB):
                acc = bank([P, CHUNK], F32)
                for kb in range(DB):
                    nc.tensor.matmul(acc[:], wk_blocks[:, kb, b, :], h[:, kb, :], start=kb == 0, stop=kb == DB - 1)
                nc.scalar.copy(k_sb[:, b, t * CHUNK : (t + 1) * CHUNK], acc[:])

        def project_v(h_t, t, s, cols):
            acc = bank([P, cols.stop - cols.start], F32)
            for kb in range(DB):
                nc.tensor.matmul(
                    acc[:], h_t[:, kb, s * P : (s + 1) * P], wv_sb[:, kb, cols], start=kb == 0, stop=kb == DB - 1
                )
            nc.vector.tensor_tensor(vT_sb[:, t * (CHUNK // P) + s, cols], acc[:], bv_sb[:, cols], ALU.add)

        def project_v_late(h_t, t, s, cols):
            acc = bank([P, cols.stop - cols.start], F32)
            nc.tensor.matmul(acc[:], shares[:], bv_terms[:, cols], start=True, stop=False)
            for kb in range(DB):
                nc.tensor.matmul(
                    acc[:], h_t[:, kb, s * P : (s + 1) * P], wv_sb[:, kb, cols], start=False, stop=kb == DB - 1
                )
            nc.scalar.copy(vT_sb[:, t * (CHUNK // P) + s, cols], acc[:])

        def softmax(tok, queries):
            nj = queries // P
            keys = slice(tok // USER * USER, (tok // USER + 1) * USER)
            scores = bank([P, nj, USER], F32)
            for jb in range(nj):
                for b in range(DB):
                    nc.tensor.matmul(
                        scores[:, jb, :],
                        q_sb[:, b, tok + jb * P : tok + (jb + 1) * P],
                        k_sb[:, b, keys],
                        start=b == 0,
                        stop=b == DB - 1,
                    )
            top = work.tile([P, nj], F32, name="top")
            nc.vector.reduce_max(top[:], scores[:], axis=AXIS.X)
            shift = work.tile([P, nj], F32, name="shift")
            nc.vector.tensor_scalar_mul(shift[:], top[:], -SCALE)
            p_sb = work.tile([P, nj, USER], BF16, name="p_sb")
            den = work.tile([P, nj], F32, name="den")
            for jb in range(nj):
                nc.scalar.activation(
                    p_sb[:, jb, :],
                    scores[:, jb, :],
                    ACT.Exp,
                    bias=shift[:, jb : jb + 1],
                    scale=SCALE,
                    accum_out=den[:, jb : jb + 1],
                )
            return tok, p_sb, den

        def flip_p(tok, p_sb):
            u, j, queries = tok // USER, tok % USER, p_sb.shape[1] * P
            pT_ps = bank([P, 2, queries], BF16)
            for nb in range(2):
                for jb in range(queries // P):
                    nc.tensor.transpose(
                        pT_ps[:, nb, jb * P : (jb + 1) * P], p_sb[:, jb, nb * P : (nb + 1) * P], ident_bf[:]
                    )
            nc.vector.tensor_copy(pT_sb[:, u, :, j : j + queries], pT_ps[:])

        def flip_r(tok, den):
            nj = den.shape[1]
            rcol = work.tile([P, nj], F32, name="rcol")
            nc.vector.reciprocal(rcol[:], den[:])
            r_ps = bank([P, nj * P], F32)
            for jb in range(nj):
                nc.tensor.transpose(
                    r_ps[:, jb * P : (jb + 1) * P], rcol[:, jb : jb + 1].to_broadcast([P, P]), ident_f[:]
                )
            nc.vector.tensor_copy(rden_sb[:, tok : tok + nj * P], r_ps[:])

        def flip(weights):
            for tok, p_sb, den in weights:
                flip_p(tok, p_sb)
            for tok, p_sb, den in weights:
                flip_r(tok, den)

        def attend_and_place(c, first_chunk, chunks=1):
            tokens = chunks * CHUNK
            tok = first_chunk * CHUNK
            num_sb = placed.tile([P, tokens], F32, name=f"num_sb{chunks}")
            for s in range(tokens // USER):
                u = tok // USER + s
                num_ps = bank([P, USER], F32)
                for nb in range(2):
                    nc.tensor.matmul(
                        num_ps[:],
                        vT_sb[:, 2 * u + nb, c * P : (c + 1) * P],
                        pT_sb[:, u, nb, :],
                        start=nb == 0,
                        stop=nb == 1,
                    )
                nc.scalar.copy(num_sb[:, s * USER : (s + 1) * USER], num_ps[:])
            nc.vector.tensor_tensor(
                window[c][:].indirect(offsets[:, tok // 16 : (tok + tokens) // 16]),
                num_sb[:],
                rden_sb[:, tok : tok + tokens],
                ALU.mult,
            )

        chunks = TOKENS // CHUNK
        blocks = range(CHUNK // P)
        h = {(0, 0): project_h(0, 0), (1, 0): project_h(1, 0)}
        project_q(h[0, 0], 0)
        h[2, 0] = project_h(2, 0)
        project_k(h[1, 0], 0)
        for t in range(chunks - 1):
            weights = [softmax(t * CHUNK + s * USER, USER) for s in range(CHUNK // USER)]
            for s in blocks:
                project_v(h[2, t], t, s, slice(0, D if t < chunks - 2 else D - P))
            flip(weights)
            h[0, t + 1] = project_h(0, t + 1)
            for c in range(DB if t < chunks - 2 else DB - 1):
                attend_and_place(c, t)
            h[1, t + 1] = project_h(1, t + 1)
            project_q(h[0, t + 1], t + 1)
            project_k(h[1, t + 1], t + 1)
            h[2, t + 1] = project_h(2, t + 1)

        t = chunks - 1
        weights = [softmax(tok, P) for tok in range(t * CHUNK, TOKENS, P)]
        for s in blocks:
            project_v(h[2, t], t, s, slice(0, P))
        flip(weights)
        for c in range(DB):
            if c == 1:
                for s in blocks:
                    project_v_late(h[2, t], t, s, slice(P, 2 * P))
            if c == 2:
                for s in blocks:
                    project_v_late(h[2, t], t, s, slice(2 * P, D))
            if c == DB - 1:
                for s in blocks:
                    project_v_late(h[2, t - 1], t - 1, s, slice(D - P, D))
                attend_and_place(c, t - 1, chunks=2)
            else:
                attend_and_place(c, t)
            nc.sync.dma_start(out[c * P : (c + 1) * P, :], window[c][:])
